import numpy as np
import ml_dtypes


def mxq(x, axis, fmt="e4m3"):
    dtype, down = {"e4m3": (ml_dtypes.float8_e4m3fn, 7), "e5m2": (ml_dtypes.float8_e5m2, 14)}[fmt]
    v = np.moveaxis(np.asarray(x, np.float32).astype(ml_dtypes.bfloat16).astype(np.float64), axis, -1)
    blocks = v.reshape(v.shape[:-1] + (-1, 32))
    amax = np.abs(blocks).max(-1, keepdims=True)
    byte = np.maximum(np.where(amax > 0, np.frexp(amax)[1] - 1 + 127, 0) - down, 1)
    scale = np.exp2(byte - 127.0)
    codes = (blocks / scale).astype(np.float32).astype(dtype).astype(np.float64)
    return np.moveaxis((codes * scale).reshape(v.shape), -1, axis)


WIDE = False


def mx_kscale(k):
    if not WIDE:
        return np.ones(k)
    levels = np.array([20, -20, 10, -10, 0])
    a = np.random.permutation(np.resize(levels, k // 512 * 4)).reshape(k // 512, 4)
    idx = np.arange(k)
    return np.exp2(a[idx // 512, idx % 128 // 32])


BF16 = ml_dtypes.bfloat16


def bf(x):
    return np.asarray(x, np.float32).astype(BF16)


def f64(x):
    return np.asarray(x).astype(np.float64)


B, N, D, H, DH = 4, 640, 1024, 16, 64
R = 2 * DH
T = B * N
EPS = 1e-12
BASE = 10000.0


def rope_tables():
    inv_freq = 1.0 / (BASE ** (np.arange(0, R, 2) / R))
    freqs = np.outer(np.arange(N), inv_freq)
    emb = np.concatenate([freqs, freqs], axis=-1)
    return np.cos(emb), np.sin(emb)


def setup_inputs():
    s = mx_kscale(T).reshape(B, N)
    gain = 0.5 * np.sqrt(DH)
    x0 = bf(np.random.standard_normal((B, N, D)))
    a = bf(np.random.standard_normal((B, N, D)))
    Wq_x = bf(np.random.standard_normal((H * DH, D)) / np.sqrt(D))
    Wq_a = bf(np.random.standard_normal((H * DH, D)) / np.sqrt(D))
    qx_scale = bf(gain * (1.0 + 0.1 * np.random.standard_normal((H, 1, DH))))
    qa_scale = bf(gain * (1.0 + 0.1 * np.random.standard_normal((H, 1, DH))))
    g = bf(np.random.standard_normal((B, H, N, R)) * np.exp2(np.random.randint(-12, 1, (B, 1, N, 1))) / s[:, None, :, None])
    p_x = f64(x0) @ f64(Wq_x).T
    return {
        "x": bf(f64(x0) * s[:, :, None]),
        "a": a,
        "Wq_x": Wq_x,
        "Wq_a": Wq_a,
        "qx_scale": qx_scale,
        "qa_scale": qa_scale,
        "p_x": np.asarray(p_x, np.float32),
        "grad_out": g,
    }


def reference(x, a, Wq_x, Wq_a, qx_scale, qa_scale, p_x, grad_out):
    g = f64(grad_out)
    cos, sin = rope_tables()
    c, sn = cos[:, :DH], sin[:, :DH]
    du = g[..., :DH] * c + g[..., DH:] * sn
    dv = du * f64(qx_scale)
    p = f64(p_x).reshape(B, N, H, DH).transpose(0, 2, 1, 3)
    r = 1.0 / np.maximum(np.sqrt(np.sum(p * p, axis=-1, keepdims=True)), EPS)
    v = p * r
    dp = (dv - v * np.sum(v * dv, axis=-1, keepdims=True)) * r
    dp = dp.transpose(0, 2, 1, 3).reshape(T, H * DH)
    return mxq(dp, 0, "e5m2").T @ mxq(f64(x).reshape(T, D), 0, "e4m3")

@@ -1,0 +1,359 @@
+import math
+
+import concourse.mybir as mybir
+
+FLOPS = 2 * 2560 * 1024 * 1024
+BYTES = 2560 * 1024 * 2 + 2560 * 1024 * 4 + 2560 * 16 * 128 * 2 + 1024 * 2 + 1024 * 1024 * 4
+
+F32 = mybir.dt.float32
+BF16 = mybir.dt.bfloat16
+I32 = mybir.dt.int32
+U32 = mybir.dt.uint32
+U8 = mybir.dt.uint8
+E4M3X4 = mybir.dt.float8_e4m3fn_x4
+E5M2X4 = mybir.dt.float8_e5m2_x4
+ALU = mybir.AluOpType
+ACT = mybir.ActivationFunctionType
+
+P = 128
+SLOTS = 4
+B, N, D, H, DH = 4, 640, 1024, 16, 64
+R = 2 * DH
+MAIN_N = P * SLOTS
+REST_P = (N - MAIN_N) // SLOTS
+PASSES = B + 1
+HEADS = 4
+CHUNK = HEADS * DH
+ROUNDS = H // HEADS
+CHUNKS = ROUNDS * PASSES
+M_TILES = CHUNK // P
+N_TILE = 512
+N_TILES = D // N_TILE
+EPS = 1e-12
+BASE = 10000.0
+ROUND_MAGIC = 1.5 * 2.0**23
+TWO_PI_HI = 6.28125
+TWO_PI_LO = 2.0 * math.pi - TWO_PI_HI
+
+
+def token_rows(c):
+    if c < B:
+        return [(0, P, c, 0, MAIN_N)]
+    return [(REST_P * b, REST_P, b, MAIN_N, N) for b in range(B)]
+
+
+def build_rotary_table(nc, consts):
+    kinds = 2 * SLOTS
+    pos_int = consts.tile([P, 2, SLOTS], I32)
+    nc.gpsimd.iota(pos_int[:, 0, :], pattern=[[1, SLOTS]], base=0, channel_multiplier=SLOTS)
+    nc.vector.tensor_single_scalar(
+        out=pos_int[:, 1, :], in_=pos_int[:, 0, :], scalar=SLOTS * REST_P - 1, op=ALU.bitwise_and
+    )
+    pos = consts.tile([P, 2, SLOTS], F32)
+    nc.vector.tensor_copy(out=pos[:, 0, :], in_=pos_int[:, 0, :])
+    nc.vector.tensor_scalar(
+        out=pos[:, 1, :], in0=pos_int[:, 1, :], scalar1=float(MAIN_N), scalar2=None, op0=ALU.add
+    )
+
+    theta = consts.tile([P, kinds, DH], F32)
+    for j in range(DH):
+        nc.vector.tensor_scalar(
+            out=theta[:, :, j],
+            in0=pos[:].rearrange("p k s -> p (k s)"),
+            scalar1=1.0 / (BASE ** (2 * j / R)),
+            scalar2=None,
+            op0=ALU.mult,
+        )
+
+    turns = consts.tile([P, kinds, DH], F32)
+    nc.vector.tensor_scalar(
+        out=turns[:], in0=theta[:], scalar1=1.0 / (2.0 * math.pi), scalar2=ROUND_MAGIC, op0=ALU.mult, op1=ALU.add
+    )
+    nc.vector.tensor_scalar(out=turns[:], in0=turns[:], scalar1=ROUND_MAGIC, scalar2=None, op0=ALU.subtract)
+    rem = consts.tile([P, kinds, DH], F32)
+    nc.vector.scalar_tensor_tensor(
+        out=rem[:], in0=turns[:], scalar=-TWO_PI_HI, in1=theta[:], op0=ALU.mult, op1=ALU.add
+    )
+    nc.vector.scalar_tensor_tensor(
+        out=rem[:], in0=turns[:], scalar=-TWO_PI_LO, in1=rem[:], op0=ALU.mult, op1=ALU.add
+    )
+
+    sin_half = consts.tile([P, kinds, DH], F32)
+    nc.scalar.activation(out=sin_half[:], in_=rem[:], func=ACT.Sin, scale=0.5)
+    quarter = consts.tile([P, kinds, DH], F32)
+    nc.vector.scalar_tensor_tensor(out=quarter[:], in0=rem[:], scalar=-1.0, in1=rem[:], op0=ALU.mult, op1=ALU.max)
+    nc.vector.tensor_scalar(
+        out=quarter[:], in0=quarter[:], scalar1=-0.5, scalar2=math.pi / 2.0, op0=ALU.mult, op1=ALU.add
+    )
+    cos_half = consts.tile([P, kinds, DH], F32)
+    nc.scalar.activation(out=cos_half[:], in_=quarter[:], func=ACT.Sin)
+
+    cos_sin = consts.tile([P, kinds, R], F32)
+    squared = consts.tile([P, kinds, DH], F32)
+    nc.vector.tensor_tensor(out=squared[:], in0=sin_half[:], in1=sin_half[:], op=ALU.mult)
+    nc.vector.tensor_scalar(
+        out=cos_sin[:, :, 0:DH], in0=squared[:], scalar1=-2.0, scalar2=1.0, op0=ALU.mult, op1=ALU.add
+    )
+    nc.vector.scalar_tensor_tensor(
+        out=cos_sin[:, :, DH:R], in0=sin_half[:], scalar=2.0, in1=cos_half[:], op0=ALU.mult, op1=ALU.mult
+    )
+    return cos_sin
+
+
+def tile_cmattention_pa_v_kernel(tc, x, a, Wq_x, Wq_a, qx_scale, qa_scale, p_x, grad_out, out):
+    nc = tc.nc
+    with (
+        tc.tile_pool(name="consts", bufs=1) as consts,
+        tc.tile_pool(name="keep", bufs=1) as keep,
+        tc.tile_pool(name="stream", bufs=2) as stream,
+        tc.psum_pool(name="psum", bufs=2) as psum,
+        tc.manual_schedule(),
+    ):
+        x_codes = keep.tile([P, PASSES, D], U32, align_bytes=64)
+        x_scales = keep.tile([P, PASSES, D], U8, align_bytes=64)
+        dp_codes = keep.tile([P, PASSES, H * DH], U32, align_bytes=64)
+        dp_scales = keep.tile([P, PASSES, H * DH], U8, align_bytes=64)
+
+        tiles = {}
+        pairs = [(h, s) for h in range(HEADS) for s in range(SLOTS)]
+
+        def dp_cols(k):
+            return slice(CHUNK * (k // PASSES), CHUNK * (k // PASSES) + CHUNK)
+
+        def load_x(c):
+            x_rows = stream.tile([P, SLOTS, D], BF16)
+            for p0, parts, b, n0, n1 in token_rows(c):
+                nc.sync.dma_start(
+                    out=x_rows[p0 : p0 + parts], in_=x[b, n0:n1, :].rearrange("(p s) d -> p s d", s=SLOTS)
+                )
+            tiles["x_rows", c] = x_rows
+
+        def regroup_x(i):
+            n_cols = slice(N_TILE * (i % N_TILES), N_TILE * (i % N_TILES) + N_TILE)
+            x_grouped = stream.tile([P, N_TILE, SLOTS], BF16, align_bytes=64)
+            nc.scalar.copy(
+                out=x_grouped[:].rearrange("p (c i) s -> p c s i", i=4),
+                in_=tiles["x_rows", i // N_TILES][:, :, n_cols].rearrange("p s (c i) -> p c s i", i=4),
+            )
+            tiles["x_grouped", i] = x_grouped
+
+        def quantise_x(i):
+            n_cols = slice(N_TILE * (i % N_TILES), N_TILE * (i % N_TILES) + N_TILE)
+            nc.vector.quantize_mx(
+                out=x_codes[:, i // N_TILES, n_cols].bitcast(E4M3X4),
+                scales=x_scales[:, i // N_TILES, n_cols],
+                in_=tiles["x_grouped", i][:].rearrange("p d s -> p (d s)"),
+            )
+
+        def load_p(k):
+            p = stream.tile([P, SLOTS, CHUNK], F32, bufs=7)
+            for p0, parts, b, n0, n1 in token_rows(k % PASSES):
+                nc.sync.dma_start(
+                    out=p[p0 : p0 + parts], in_=p_x[b, n0:n1, dp_cols(k)].rearrange("(p s) k -> p s k", s=SLOTS)
+                )
+            tiles["p", k] = p
+
+        def load_g(k):
+            h0 = HEADS * (k // PASSES)
+            g = stream.tile([P, HEADS, SLOTS, R], BF16, bufs=3)
+            for p0, parts, b, n0, n1 in token_rows(k % PASSES):
+                nc.sync.dma_start(
+                    out=g[p0 : p0 + parts],
+                    in_=grad_out[b, h0 : h0 + HEADS, n0:n1, :].rearrange("h (p s) k -> p h s k", s=SLOTS),
+                )
+            tiles["g", k] = g
+
+        def sum_squares(k):
+            norm2 = stream.tile([P, HEADS * SLOTS], F32, bufs=3)
+            for i, (h, s) in enumerate(pairs):
+                unused = stream.tile([P, DH], BF16, name="unused")
+                nc.scalar.activation(
+                    out=unused[:],
+                    in_=tiles["p", k][:, s, DH * h : DH * h + DH],
+                    func=ACT.Square,
+                    accum_out=norm2[:, i : i + 1],
+                )
+            tiles["norm2", k] = norm2
+
+        def clamp_norm(k):
+            inv_a = stream.tile([P, HEADS * SLOTS], F32, bufs=4)
+            nc.vector.tensor_scalar(
+                out=inv_a[:], in0=tiles["norm2", k][:], scalar1=EPS * EPS, scalar2=None, op0=ALU.max
+            )
+            tiles["inv_a", k] = inv_a
+
+        def invert_norm(k):
+            nc.vector.reciprocal(out=tiles["inv_a", k][:], in_=tiles["inv_a", k][:])
+
+        def root(k):
+            rho = stream.tile([P, HEADS * SLOTS], F32)
+            nc.scalar.activation(out=rho[:], in_=tiles["inv_a", k][:], func=ACT.Sqrt)
+            tiles["rho", k] = rho
+
+        def gain_of(k, shape_like_slots):
+            by_head = gain[:, dp_cols(k)].rearrange("p (h j) -> p h j", h=HEADS)
+            if shape_like_slots:
+                return by_head.unsqueeze(1).to_broadcast([P, SLOTS, HEADS, DH])
+            return by_head.unsqueeze(2).to_broadcast([P, HEADS, SLOTS, DH])
+
+        def fold_gain(r):
+            folded = stream.tile([P, SLOTS, HEADS, R], F32)
+            for half in range(2):
+                nc.vector.tensor_tensor(
+                    out=folded[:, :, :, DH * half : DH * half + DH],
+                    in0=cos_sin[:, 0:SLOTS, DH * half : DH * half + DH].unsqueeze(2).to_broadcast([P, SLOTS, HEADS, DH]),
+                    in1=gain_of(PASSES * r, True),
+                    op=ALU.mult,
+                )
+            tiles["folded", r] = folded
+
+        def turn(k):
+            turned = stream.tile([P, HEADS, SLOTS, R], F32)
+            for i, (h, s) in enumerate(pairs):
+                if k % PASSES < B:
+                    table = tiles["folded", k // PASSES][:, s, h, :]
+                else:
+                    table = cos_sin[:, SLOTS + s, :]
+                nc.vector.scalar_tensor_tensor(
+                    out=turned[:, h, s, :],
+                    in0=tiles["g", k][:, h, s, :],
+                    scalar=tiles["rho", k][:, i : i + 1],
+                    in1=table,
+                    op0=ALU.mult,
+                    op1=ALU.mult,
+                )
+            tiles["turned", k] = turned
+
+        def add_halves(k):
+            dv = stream.tile([P, HEADS, SLOTS, DH], F32, bufs=3)
+            turned = tiles["turned", k]
+            nc.vector.tensor_tensor(out=dv[:], in0=turned[:, :, :, 0:DH], in1=turned[:, :, :, DH:R], op=ALU.add)
+            tiles["dv", k] = dv
+
+        def apply_gain(k):
+            nc.vector.tensor_tensor(out=tiles["dv", k][:], in0=tiles["dv", k][:], in1=gain_of(k, False), op=ALU.mult)
+
+        def times_p(k):
+            prod = stream.tile([P, HEADS, SLOTS, DH], F32)
+            nc.vector.tensor_tensor(
+                out=prod[:],
+                in0=tiles["p", k][:].rearrange("p s (h j) -> p h s j", h=HEADS),
+                in1=tiles["dv", k][:],
+                op=ALU.mult,
+            )
+            tiles["prod", k] = prod
+
+        def dot_products(k):
+            dot = stream.tile([P, HEADS * SLOTS], F32)
+            for i, (h, s) in enumerate(pairs):
+                unused = stream.tile([P, DH], BF16, name="unused")
+                nc.scalar.activation(
+                    out=unused[:], in_=tiles["prod", k][:, h, s, :], func=ACT.Copy, accum_out=dot[:, i : i + 1]
+                )
+            tiles["dot", k] = dot
+
+        def projection(k):
+            back = stream.tile([P, HEADS * SLOTS], F32)
+            nc.vector.scalar_tensor_tensor(
+                out=back[:], in0=tiles["dot", k][:], scalar=-1.0, in1=tiles["inv_a", k][:], op0=ALU.mult, op1=ALU.mult
+            )
+            tiles["back", k] = back
+
+        def along_p(k):
+            along = stream.tile([P, HEADS, SLOTS, DH], F32)
+            for i, (h, s) in enumerate(pairs):
+                nc.scalar.activation(
+                    out=along[:, h, s, :],
+                    in_=tiles["p", k][:, s, DH * h : DH * h + DH],
+                    func=ACT.Copy,
+                    scale=tiles["back", k][:, i : i + 1],
+                )
+            tiles["along", k] = along
+
+        def round_dp(k):
+            dp = stream.tile([P, CHUNK * SLOTS], BF16, align_bytes=64)
+            nc.vector.tensor_tensor(
+                out=dp[:].rearrange("p (h j s) -> p h j s", h=HEADS, s=SLOTS),
+                in0=tiles["dv", k][:].rearrange("p h s j -> p h j s"),
+                in1=tiles["along", k][:].rearrange("p h s j -> p h j s"),
+                op=ALU.add,
+            )
+            tiles["dp", k] = dp
+
+        def quantise_dp(k):
+            nc.vector.quantize_mx(
+                out=dp_codes[:, k % PASSES, dp_cols(k)].bitcast(E5M2X4),
+                scales=dp_scales[:, k % PASSES, dp_cols(k)],
+                in_=tiles["dp", k][:],
+            )
+
+        def multiply(k):
+            r, c = k // PASSES, k % PASSES
+            for m in range(M_TILES):
+                rows = slice(CHUNK * r + P * m, CHUNK * r + P * m + P)
+                for n in range(N_TILES):
+                    if c == 0:
+                        tiles["sum", r, m, n] = psum.tile([P, N_TILE], F32, name="sum_%d_%d" % (m, n))
+                    n_cols = slice(N_TILE * n, N_TILE * n + N_TILE)
+                    nc.tensor.matmul_mx(
+                        out=tiles["sum", r, m, n][:],
+                        lhsT=dp_codes[:, c, rows].bitcast(E5M2X4),
+                        lhsT_scale=dp_scales[:, c, rows],
+                        rhs=x_codes[:, c, n_cols].bitcast(E4M3X4),
+                        rhs_scale=x_scales[:, c, n_cols],
+                        start=(c == 0),
+                        stop=(c == PASSES - 1),
+                    )
+
+        def store_round(r):
+            for m in range(M_TILES):
+                rows = slice(CHUNK * r + P * m, CHUNK * r + P * m + P)
+                result = stream.tile([P, D], F32)
+                for n in range(N_TILES):
+                    nc.scalar.copy(out=result[:, N_TILE * n : N_TILE * n + N_TILE], in_=tiles["sum", r, m, n][:])
+                nc.sync.dma_start(out=out[rows, :], in_=result[:])
+
+        def when_live(stage, k, count):
+            if 0 <= k < count:
+                stage(k)
+
+        def step(t):
+            when_live(load_p, t + 4, CHUNKS)
+            if t % 2 == 0:
+                when_live(load_x, t // 2 + 1, PASSES)
+            when_live(load_g, t + 2, CHUNKS)
+
+            when_live(along_p, t - 2, CHUNKS)
+            when_live(dot_products, t - 1, CHUNKS)
+            when_live(root, t + 1, CHUNKS)
+            when_live(sum_squares, t + 3, CHUNKS)
+            when_live(regroup_x, t, PASSES * N_TILES)
+
+            when_live(turn, t, CHUNKS)
+            when_live(round_dp, t - 2, CHUNKS)
+            when_live(add_halves, t, CHUNKS)
+            when_live(quantise_dp, t - 2, CHUNKS)
+            if t % PASSES == B:
+                when_live(apply_gain, t, CHUNKS)
+            when_live(clamp_norm, t + 2, CHUNKS)
+            when_live(times_p, t, CHUNKS)
+            when_live(invert_norm, t + 2, CHUNKS)
+            if (t + 1) % PASSES == 0:
+                when_live(fold_gain, (t + 1) // PASSES, ROUNDS)
+            when_live(quantise_x, t - 1, PASSES * N_TILES)
+            when_live(projection, t - 1, CHUNKS)
+
+            if t % 2 == 0:
+                when_live(multiply, t // 2 - 1, PASSES)
+            if t - 2 >= PASSES:
+                when_live(multiply, t - 2, CHUNKS)
+            if t % PASSES == 1:
+                when_live(store_round, t // PASSES - 2, ROUNDS)
+
+        gain = consts.tile([P, H * DH], BF16)
+        step(-4)
+        step(-3)
+        nc.sync.dma_start(out=gain[:], in_=qx_scale.rearrange("h o j -> (h o j)").partition_broadcast(P))
+        cos_sin = build_rotary_table(nc, consts)
+        for t in range(-2, PASSES * (ROUNDS + 2) + 2):
+            step(t)

@@ -29,6 +29,7 @@ CHUNKS = ROUNDS * PASSES
 M_TILES = CHUNK // P
 N_TILE = 512
 N_TILES = D // N_TILE
+RUN = 4
 EPS = 1e-12
 BASE = 10000.0
 ROUND_MAGIC = 1.5 * 2.0**23
@@ -115,7 +116,7 @@ def tile_cmattention_pa_v_kernel(tc, x, a, Wq_x, Wq_a, qx_scale, qa_scale, p_x, 
         dp_scales = keep.tile([P, PASSES, H * DH], U8, align_bytes=64)
 
         tiles = {}
-        pairs = [(h, s) for h in range(HEADS) for s in range(SLOTS)]
+        pairs = [(s, h, slice(DH * h, DH * h + DH)) for s in range(SLOTS) for h in range(HEADS)]
 
         def dp_cols(k):
             return slice(CHUNK * (k // PASSES), CHUNK * (k // PASSES) + CHUNK)
@@ -130,10 +131,10 @@ def tile_cmattention_pa_v_kernel(tc, x, a, Wq_x, Wq_a, qx_scale, qa_scale, p_x, 
 
         def regroup_x(i):
             n_cols = slice(N_TILE * (i % N_TILES), N_TILE * (i % N_TILES) + N_TILE)
-            x_grouped = stream.tile([P, N_TILE, SLOTS], BF16, align_bytes=64)
+            x_grouped = stream.tile([P, N_TILE * SLOTS], BF16, align_bytes=64)
             nc.scalar.copy(
-                out=x_grouped[:].rearrange("p (c i) s -> p c s i", i=4),
-                in_=tiles["x_rows", i // N_TILES][:, :, n_cols].rearrange("p s (c i) -> p c s i", i=4),
+                out=x_grouped[:].rearrange("p (c i s) -> p c s i", i=RUN, s=SLOTS),
+                in_=tiles["x_rows", i // N_TILES][:, :, n_cols].rearrange("p s (c i) -> p c s i", i=RUN),
             )
             tiles["x_grouped", i] = x_grouped
 
@@ -142,7 +143,7 @@ def tile_cmattention_pa_v_kernel(tc, x, a, Wq_x, Wq_a, qx_scale, qa_scale, p_x, 
             nc.vector.quantize_mx(
                 out=x_codes[:, i // N_TILES, n_cols].bitcast(E4M3X4),
                 scales=x_scales[:, i // N_TILES, n_cols],
-                in_=tiles["x_grouped", i][:].rearrange("p d s -> p (d s)"),
+                in_=tiles["x_grouped", i][:],
             )
 
         def load_p(k):
@@ -164,37 +165,31 @@ def tile_cmattention_pa_v_kernel(tc, x, a, Wq_x, Wq_a, qx_scale, qa_scale, p_x, 
             tiles["g", k] = g
 
         def sum_squares(k):
-            norm2 = stream.tile([P, HEADS * SLOTS], F32, bufs=3)
-            for i, (h, s) in enumerate(pairs):
+            norm2 = stream.tile([P, SLOTS * HEADS], F32, bufs=3)
+            for i, (s, h, cols) in enumerate(pairs):
                 unused = stream.tile([P, DH], BF16, name="unused")
                 nc.scalar.activation(
-                    out=unused[:],
-                    in_=tiles["p", k][:, s, DH * h : DH * h + DH],
-                    func=ACT.Square,
-                    accum_out=norm2[:, i : i + 1],
+                    out=unused[:], in_=tiles["p", k][:, s, cols], func=ACT.Square, accum_out=norm2[:, i : i + 1]
                 )
             tiles["norm2", k] = norm2
 
         def clamp_norm(k):
-            inv_a = stream.tile([P, HEADS * SLOTS], F32, bufs=4)
+            minus_inv = stream.tile([P, SLOTS * HEADS], F32, bufs=5)
             nc.vector.tensor_scalar(
-                out=inv_a[:], in0=tiles["norm2", k][:], scalar1=EPS * EPS, scalar2=None, op0=ALU.max
+                out=minus_inv[:], in0=tiles["norm2", k][:], scalar1=EPS * EPS, scalar2=-1.0, op0=ALU.max, op1=ALU.mult
             )
-            tiles["inv_a", k] = inv_a
+            tiles["minus_inv", k] = minus_inv
 
         def invert_norm(k):
-            nc.vector.reciprocal(out=tiles["inv_a", k][:], in_=tiles["inv_a", k][:])
+            nc.vector.reciprocal(out=tiles["minus_inv", k][:], in_=tiles["minus_inv", k][:])
 
         def root(k):
-            rho = stream.tile([P, HEADS * SLOTS], F32)
-            nc.scalar.activation(out=rho[:], in_=tiles["inv_a", k][:], func=ACT.Sqrt)
+            rho = stream.tile([P, SLOTS * HEADS], F32)
+            nc.scalar.activation(out=rho[:], in_=tiles["minus_inv", k][:], func=ACT.Sqrt, scale=-1.0)
             tiles["rho", k] = rho
 
-        def gain_of(k, shape_like_slots):
-            by_head = gain[:, dp_cols(k)].rearrange("p (h j) -> p h j", h=HEADS)
-            if shape_like_slots:
-                return by_head.unsqueeze(1).to_broadcast([P, SLOTS, HEADS, DH])
-            return by_head.unsqueeze(2).to_broadcast([P, HEADS, SLOTS, DH])
+        def gain_of(k):
+            return gain[:, dp_cols(k)].unsqueeze(1).to_broadcast([P, SLOTS, CHUNK])
 
         def fold_gain(r):
             folded = stream.tile([P, SLOTS, HEADS, R], F32)
@@ -202,20 +197,20 @@ def tile_cmattention_pa_v_kernel(tc, x, a, Wq_x, Wq_a, qx_scale, qa_scale, p_x, 
                 nc.vector.tensor_tensor(
                     out=folded[:, :, :, DH * half : DH * half + DH],
                     in0=cos_sin[:, 0:SLOTS, DH * half : DH * half + DH].unsqueeze(2).to_broadcast([P, SLOTS, HEADS, DH]),
-                    in1=gain_of(PASSES * r, True),
+                    in1=gain_of(PASSES * r).rearrange("p s (h j) -> p s h j", h=HEADS),
                     op=ALU.mult,
                 )
             tiles["folded", r] = folded
 
         def turn(k):
-            turned = stream.tile([P, HEADS, SLOTS, R], F32)
-            for i, (h, s) in enumerate(pairs):
+            turned = stream.tile([P, SLOTS, HEADS, R], F32)
+            for i, (s, h, cols) in enumerate(pairs):
                 if k % PASSES < B:
                     table = tiles["folded", k // PASSES][:, s, h, :]
                 else:
                     table = cos_sin[:, SLOTS + s, :]
                 nc.vector.scalar_tensor_tensor(
-                    out=turned[:, h, s, :],
+                    out=turned[:, s, h, :],
                     in0=tiles["g", k][:, h, s, :],
                     scalar=tiles["rho", k][:, i : i + 1],
                     in1=table,
@@ -225,57 +220,48 @@ def tile_cmattention_pa_v_kernel(tc, x, a, Wq_x, Wq_a, qx_scale, qa_scale, p_x, 
             tiles["turned", k] = turned
 
         def add_halves(k):
-            dv = stream.tile([P, HEADS, SLOTS, DH], F32, bufs=3)
+            dv = stream.tile([P, SLOTS, CHUNK], F32)
             turned = tiles["turned", k]
-            nc.vector.tensor_tensor(out=dv[:], in0=turned[:, :, :, 0:DH], in1=turned[:, :, :, DH:R], op=ALU.add)
+            nc.vector.tensor_tensor(
+                out=dv[:].rearrange("p s (h j) -> p s h j", h=HEADS),
+                in0=turned[:, :, :, 0:DH],
+                in1=turned[:, :, :, DH:R],
+                op=ALU.add,
+            )
             tiles["dv", k] = dv
 
         def apply_gain(k):
-            nc.vector.tensor_tensor(out=tiles["dv", k][:], in0=tiles["dv", k][:], in1=gain_of(k, False), op=ALU.mult)
+            nc.vector.tensor_tensor(out=tiles["dv", k][:], in0=tiles["dv", k][:], in1=gain_of(k), op=ALU.mult)
 
         def times_p(k):
-            prod = stream.tile([P, HEADS, SLOTS, DH], F32)
-            nc.vector.tensor_tensor(
-                out=prod[:],
-                in0=tiles["p", k][:].rearrange("p s (h j) -> p h s j", h=HEADS),
-                in1=tiles["dv", k][:],
-                op=ALU.mult,
-            )
+            prod = stream.tile([P, SLOTS, CHUNK], F32)
+            nc.vector.tensor_tensor(out=prod[:], in0=tiles["p", k][:], in1=tiles["dv", k][:], op=ALU.mult)
             tiles["prod", k] = prod
 
-        def dot_products(k):
-            dot = stream.tile([P, HEADS * SLOTS], F32)
-            for i, (h, s) in enumerate(pairs):
+        def project(k):
+            back = stream.tile([P, SLOTS * HEADS], F32)
+            for i, (s, h, cols) in enumerate(pairs):
                 unused = stream.tile([P, DH], BF16, name="unused")
                 nc.scalar.activation(
-                    out=unused[:], in_=tiles["prod", k][:, h, s, :], func=ACT.Copy, accum_out=dot[:, i : i + 1]
-                )
-            tiles["dot", k] = dot
-
-        def projection(k):
-            back = stream.tile([P, HEADS * SLOTS], F32)
-            nc.vector.scalar_tensor_tensor(
-                out=back[:], in0=tiles["dot", k][:], scalar=-1.0, in1=tiles["inv_a", k][:], op0=ALU.mult, op1=ALU.mult
-            )
-            tiles["back", k] = back
-
-        def along_p(k):
-            along = stream.tile([P, HEADS, SLOTS, DH], F32)
-            for i, (h, s) in enumerate(pairs):
-                nc.scalar.activation(
-                    out=along[:, h, s, :],
-                    in_=tiles["p", k][:, s, DH * h : DH * h + DH],
+                    out=unused[:],
+                    in_=tiles["prod", k][:, s, cols],
                     func=ACT.Copy,
-                    scale=tiles["back", k][:, i : i + 1],
+                    scale=tiles["minus_inv", k][:, i : i + 1],
+                    accum_out=back[:, i : i + 1],
+                )
+            along = stream.tile([P, SLOTS, CHUNK], F32)
+            for i, (s, h, cols) in enumerate(pairs):
+                nc.scalar.activation(
+                    out=along[:, s, cols], in_=tiles["p", k][:, s, cols], func=ACT.Copy, scale=back[:, i : i + 1]
                 )
             tiles["along", k] = along
 
         def round_dp(k):
             dp = stream.tile([P, CHUNK * SLOTS], BF16, align_bytes=64)
             nc.vector.tensor_tensor(
-                out=dp[:].rearrange("p (h j s) -> p h j s", h=HEADS, s=SLOTS),
-                in0=tiles["dv", k][:].rearrange("p h s j -> p h j s"),
-                in1=tiles["along", k][:].rearrange("p h s j -> p h j s"),
+                out=dp[:].rearrange("p (c i s) -> p c s i", i=RUN, s=SLOTS),
+                in0=tiles["dv", k][:].rearrange("p s (c i) -> p c s i", i=RUN),
+                in1=tiles["along", k][:].rearrange("p s (c i) -> p c s i", i=RUN),
                 op=ALU.add,
             )
             tiles["dp", k] = dp
@@ -318,30 +304,28 @@ def tile_cmattention_pa_v_kernel(tc, x, a, Wq_x, Wq_a, qx_scale, qa_scale, p_x, 
                 stage(k)
 
         def step(t):
-            when_live(load_p, t + 4, CHUNKS)
+            when_live(load_p, t + 5, CHUNKS)
             if t % 2 == 0:
                 when_live(load_x, t // 2 + 1, PASSES)
             when_live(load_g, t + 2, CHUNKS)
 
-            when_live(along_p, t - 2, CHUNKS)
-            when_live(dot_products, t - 1, CHUNKS)
+            when_live(project, t - 1, CHUNKS)
             when_live(root, t + 1, CHUNKS)
-            when_live(sum_squares, t + 3, CHUNKS)
+            when_live(sum_squares, t + 4, CHUNKS)
             when_live(regroup_x, t, PASSES * N_TILES)
 
             when_live(turn, t, CHUNKS)
-            when_live(round_dp, t - 2, CHUNKS)
-            when_live(add_halves, t, CHUNKS)
             when_live(quantise_dp, t - 2, CHUNKS)
+            when_live(add_halves, t, CHUNKS)
+            when_live(clamp_norm, t + 3, CHUNKS)
+            when_live(invert_norm, t + 2, CHUNKS)
             if t % PASSES == B:
                 when_live(apply_gain, t, CHUNKS)
-            when_live(clamp_norm, t + 2, CHUNKS)
+            when_live(quantise_x, t - 1, PASSES * N_TILES)
             when_live(times_p, t, CHUNKS)
-            when_live(invert_norm, t + 2, CHUNKS)
             if (t + 1) % PASSES == 0:
                 when_live(fold_gain, (t + 1) // PASSES, ROUNDS)
-            when_live(quantise_x, t - 1, PASSES * N_TILES)
-            when_live(projection, t - 1, CHUNKS)
+            when_live(round_dp, t - 1, CHUNKS)
 
             if t % 2 == 0:
                 when_live(multiply, t // 2 - 1, PASSES)
@@ -351,9 +335,9 @@ def tile_cmattention_pa_v_kernel(tc, x, a, Wq_x, Wq_a, qx_scale, qa_scale, p_x, 
                 when_live(store_round, t // PASSES - 2, ROUNDS)
 
         gain = consts.tile([P, H * DH], BF16)
+        step(-5)
         step(-4)
-        step(-3)
         nc.sync.dma_start(out=gain[:], in_=qx_scale.rearrange("h o j -> (h o j)").partition_broadcast(P))
         cos_sin = build_rotary_table(nc, consts)
-        for t in range(-2, PASSES * (ROUNDS + 2) + 2):
+        for t in range(-3, PASSES * (ROUNDS + 2) + 2):
             step(t)

@@ -132,10 +132,12 @@ def tile_cmattention_pa_v_kernel(tc, x, a, Wq_x, Wq_a, qx_scale, qa_scale, p_x, 
         def regroup_x(i):
             n_cols = slice(N_TILE * (i % N_TILES), N_TILE * (i % N_TILES) + N_TILE)
             x_grouped = stream.tile([P, N_TILE * SLOTS], BF16, align_bytes=64)
-            nc.scalar.copy(
-                out=x_grouped[:].rearrange("p (c i s) -> p c s i", i=RUN, s=SLOTS),
-                in_=tiles["x_rows", i // N_TILES][:, :, n_cols].rearrange("p s (c i) -> p c s i", i=RUN),
-            )
+            side_by_side = x_grouped[:].rearrange("p (c i s) -> p c s i", i=RUN, s=SLOTS)
+            by_slot = tiles["x_rows", i // N_TILES][:, :, n_cols].rearrange("p s (c i) -> p c s i", i=RUN)
+            if i % 2 == 0:
+                nc.scalar.copy(out=side_by_side, in_=by_slot)
+            else:
+                nc.vector.tensor_copy(out=side_by_side, in_=by_slot)
             tiles["x_grouped", i] = x_grouped
 
         def quantise_x(i):
@@ -166,10 +168,10 @@ def tile_cmattention_pa_v_kernel(tc, x, a, Wq_x, Wq_a, qx_scale, qa_scale, p_x, 
 
         def sum_squares(k):
             norm2 = stream.tile([P, SLOTS * HEADS], F32, bufs=3)
+            squares = stream.tile([P, SLOTS, CHUNK], BF16)
             for i, (s, h, cols) in enumerate(pairs):
-                unused = stream.tile([P, DH], BF16, name="unused")
                 nc.scalar.activation(
-                    out=unused[:], in_=tiles["p", k][:, s, cols], func=ACT.Square, accum_out=norm2[:, i : i + 1]
+                    out=squares[:, s, cols], in_=tiles["p", k][:, s, cols], func=ACT.Square, accum_out=norm2[:, i : i + 1]
                 )
             tiles["norm2", k] = norm2
 
@@ -184,46 +186,46 @@ def tile_cmattention_pa_v_kernel(tc, x, a, Wq_x, Wq_a, qx_scale, qa_scale, p_x, 
             nc.vector.reciprocal(out=tiles["minus_inv", k][:], in_=tiles["minus_inv", k][:])
 
         def root(k):
-            rho = stream.tile([P, SLOTS * HEADS], F32)
+            rho = stream.tile([P, SLOTS * HEADS], F32, bufs=3)
             nc.scalar.activation(out=rho[:], in_=tiles["minus_inv", k][:], func=ACT.Sqrt, scale=-1.0)
             tiles["rho", k] = rho
+
+        def cube(k):
+            minus_rho3 = stream.tile([P, SLOTS * HEADS], F32, bufs=3)
+            nc.vector.tensor_tensor(out=minus_rho3[:], in0=tiles["rho", k][:], in1=tiles["minus_inv", k][:], op=ALU.mult)
+            tiles["minus_rho3", k] = minus_rho3
 
         def gain_of(k):
             return gain[:, dp_cols(k)].unsqueeze(1).to_broadcast([P, SLOTS, CHUNK])
 
         def fold_gain(r):
-            folded = stream.tile([P, SLOTS, HEADS, R], F32)
+            folded = stream.tile([P, HEADS, SLOTS, R], F32)
             for half in range(2):
                 nc.vector.tensor_tensor(
                     out=folded[:, :, :, DH * half : DH * half + DH],
-                    in0=cos_sin[:, 0:SLOTS, DH * half : DH * half + DH].unsqueeze(2).to_broadcast([P, SLOTS, HEADS, DH]),
-                    in1=gain_of(PASSES * r).rearrange("p s (h j) -> p s h j", h=HEADS),
+                    in0=cos_sin[:, 0:SLOTS, DH * half : DH * half + DH].unsqueeze(1).to_broadcast([P, HEADS, SLOTS, DH]),
+                    in1=gain[:, dp_cols(PASSES * r)]
+                    .rearrange("p (h j) -> p h j", h=HEADS)
+                    .unsqueeze(2)
+                    .to_broadcast([P, HEADS, SLOTS, DH]),
                     op=ALU.mult,
                 )
             tiles["folded", r] = folded
 
         def turn(k):
-            turned = stream.tile([P, SLOTS, HEADS, R], F32)
-            for i, (s, h, cols) in enumerate(pairs):
-                if k % PASSES < B:
-                    table = tiles["folded", k // PASSES][:, s, h, :]
-                else:
-                    table = cos_sin[:, SLOTS + s, :]
-                nc.vector.scalar_tensor_tensor(
-                    out=turned[:, s, h, :],
-                    in0=tiles["g", k][:, h, s, :],
-                    scalar=tiles["rho", k][:, i : i + 1],
-                    in1=table,
-                    op0=ALU.mult,
-                    op1=ALU.mult,
-                )
+            turned = stream.tile([P, HEADS, SLOTS, R], F32)
+            if k % PASSES < B:
+                table = tiles["folded", k // PASSES][:]
+            else:
+                table = cos_sin[:, SLOTS : 2 * SLOTS, :].unsqueeze(1).to_broadcast([P, HEADS, SLOTS, R])
+            nc.vector.tensor_tensor(out=turned[:], in0=tiles["g", k][:], in1=table, op=ALU.mult)
             tiles["turned", k] = turned
 
         def add_halves(k):
             dv = stream.tile([P, SLOTS, CHUNK], F32)
             turned = tiles["turned", k]
             nc.vector.tensor_tensor(
-                out=dv[:].rearrange("p s (h j) -> p s h j", h=HEADS),
+                out=dv[:].rearrange("p s (h j) -> p h s j", h=HEADS),
                 in0=turned[:, :, :, 0:DH],
                 in1=turned[:, :, :, DH:R],
                 op=ALU.add,
@@ -238,15 +240,22 @@ def tile_cmattention_pa_v_kernel(tc, x, a, Wq_x, Wq_a, qx_scale, qa_scale, p_x, 
             nc.vector.tensor_tensor(out=prod[:], in0=tiles["p", k][:], in1=tiles["dv", k][:], op=ALU.mult)
             tiles["prod", k] = prod
 
+        def scale_dv(k):
+            scaled = stream.tile([P, SLOTS, CHUNK], F32)
+            for i, (s, h, cols) in enumerate(pairs):
+                nc.scalar.activation(
+                    out=scaled[:, s, cols], in_=tiles["dv", k][:, s, cols], func=ACT.Copy, scale=tiles["rho", k][:, i : i + 1]
+                )
+            tiles["scaled", k] = scaled
+
         def project(k):
             back = stream.tile([P, SLOTS * HEADS], F32)
             for i, (s, h, cols) in enumerate(pairs):
-                unused = stream.tile([P, DH], BF16, name="unused")
                 nc.scalar.activation(
-                    out=unused[:],
+                    out=tiles["prod", k][:, s, cols],
                     in_=tiles["prod", k][:, s, cols],
                     func=ACT.Copy,
-                    scale=tiles["minus_inv", k][:, i : i + 1],
+                    scale=tiles["minus_rho3", k][:, i : i + 1],
                     accum_out=back[:, i : i + 1],
                 )
             along = stream.tile([P, SLOTS, CHUNK], F32)
@@ -260,7 +269,7 @@ def tile_cmattention_pa_v_kernel(tc, x, a, Wq_x, Wq_a, qx_scale, qa_scale, p_x, 
             dp = stream.tile([P, CHUNK * SLOTS], BF16, align_bytes=64)
             nc.vector.tensor_tensor(
                 out=dp[:].rearrange("p (c i s) -> p c s i", i=RUN, s=SLOTS),
-                in0=tiles["dv", k][:].rearrange("p s (c i) -> p c s i", i=RUN),
+                in0=tiles["scaled", k][:].rearrange("p s (c i) -> p c s i", i=RUN),
                 in1=tiles["along", k][:].rearrange("p s (c i) -> p c s i", i=RUN),
                 op=ALU.add,
             )
@@ -296,7 +305,11 @@ def tile_cmattention_pa_v_kernel(tc, x, a, Wq_x, Wq_a, qx_scale, qa_scale, p_x, 
                 rows = slice(CHUNK * r + P * m, CHUNK * r + P * m + P)
                 result = stream.tile([P, D], F32)
                 for n in range(N_TILES):
-                    nc.scalar.copy(out=result[:, N_TILE * n : N_TILE * n + N_TILE], in_=tiles["sum", r, m, n][:])
+                    n_cols = slice(N_TILE * n, N_TILE * n + N_TILE)
+                    if m == 0:
+                        nc.scalar.copy(out=result[:, n_cols], in_=tiles["sum", r, m, n][:])
+                    else:
+                        nc.vector.tensor_copy(out=result[:, n_cols], in_=tiles["sum", r, m, n][:])
                 nc.sync.dma_start(out=out[rows, :], in_=result[:])
 
         def when_live(stage, k, count):
@@ -309,19 +322,24 @@ def tile_cmattention_pa_v_kernel(tc, x, a, Wq_x, Wq_a, qx_scale, qa_scale, p_x, 
                 when_live(load_x, t // 2 + 1, PASSES)
             when_live(load_g, t + 2, CHUNKS)
 
+            when_live(scale_dv, t - 1, CHUNKS)
             when_live(project, t - 1, CHUNKS)
             when_live(root, t + 1, CHUNKS)
             when_live(sum_squares, t + 4, CHUNKS)
-            when_live(regroup_x, t, PASSES * N_TILES)
+            if t % 2 == 0:
+                when_live(regroup_x, t, PASSES * N_TILES)
 
             when_live(turn, t, CHUNKS)
             when_live(quantise_dp, t - 2, CHUNKS)
             when_live(add_halves, t, CHUNKS)
             when_live(clamp_norm, t + 3, CHUNKS)
             when_live(invert_norm, t + 2, CHUNKS)
+            when_live(cube, t, CHUNKS)
             if t % PASSES == B:
                 when_live(apply_gain, t, CHUNKS)
             when_live(quantise_x, t - 1, PASSES * N_TILES)
+            if t % 2 == 1:
+                when_live(regroup_x, t, PASSES * N_TILES)
             when_live(times_p, t, CHUNKS)
             if (t + 1) % PASSES == 0:
                 when_live(fold_gain, (t + 1) // PASSES, ROUNDS)

@@ -132,12 +132,10 @@ def tile_cmattention_pa_v_kernel(tc, x, a, Wq_x, Wq_a, qx_scale, qa_scale, p_x, 
         def regroup_x(i):
             n_cols = slice(N_TILE * (i % N_TILES), N_TILE * (i % N_TILES) + N_TILE)
             x_grouped = stream.tile([P, N_TILE * SLOTS], BF16, align_bytes=64)
-            side_by_side = x_grouped[:].rearrange("p (c i s) -> p c s i", i=RUN, s=SLOTS)
-            by_slot = tiles["x_rows", i // N_TILES][:, :, n_cols].rearrange("p s (c i) -> p c s i", i=RUN)
-            if i % 2 == 0:
-                nc.scalar.copy(out=side_by_side, in_=by_slot)
-            else:
-                nc.vector.tensor_copy(out=side_by_side, in_=by_slot)
+            nc.scalar.copy(
+                out=x_grouped[:].rearrange("p (c i s) -> p c s i", i=RUN, s=SLOTS),
+                in_=tiles["x_rows", i // N_TILES][:, :, n_cols].rearrange("p s (c i) -> p c s i", i=RUN),
+            )
             tiles["x_grouped", i] = x_grouped
 
         def quantise_x(i):
@@ -186,46 +184,46 @@ def tile_cmattention_pa_v_kernel(tc, x, a, Wq_x, Wq_a, qx_scale, qa_scale, p_x, 
             nc.vector.reciprocal(out=tiles["minus_inv", k][:], in_=tiles["minus_inv", k][:])
 
         def root(k):
-            rho = stream.tile([P, SLOTS * HEADS], F32, bufs=3)
+            rho = stream.tile([P, SLOTS * HEADS], F32)
             nc.scalar.activation(out=rho[:], in_=tiles["minus_inv", k][:], func=ACT.Sqrt, scale=-1.0)
             tiles["rho", k] = rho
-
-        def cube(k):
-            minus_rho3 = stream.tile([P, SLOTS * HEADS], F32, bufs=3)
-            nc.vector.tensor_tensor(out=minus_rho3[:], in0=tiles["rho", k][:], in1=tiles["minus_inv", k][:], op=ALU.mult)
-            tiles["minus_rho3", k] = minus_rho3
 
         def gain_of(k):
             return gain[:, dp_cols(k)].unsqueeze(1).to_broadcast([P, SLOTS, CHUNK])
 
         def fold_gain(r):
-            folded = stream.tile([P, HEADS, SLOTS, R], F32)
+            folded = stream.tile([P, SLOTS, HEADS, R], F32)
             for half in range(2):
                 nc.vector.tensor_tensor(
                     out=folded[:, :, :, DH * half : DH * half + DH],
-                    in0=cos_sin[:, 0:SLOTS, DH * half : DH * half + DH].unsqueeze(1).to_broadcast([P, HEADS, SLOTS, DH]),
-                    in1=gain[:, dp_cols(PASSES * r)]
-                    .rearrange("p (h j) -> p h j", h=HEADS)
-                    .unsqueeze(2)
-                    .to_broadcast([P, HEADS, SLOTS, DH]),
+                    in0=cos_sin[:, 0:SLOTS, DH * half : DH * half + DH].unsqueeze(2).to_broadcast([P, SLOTS, HEADS, DH]),
+                    in1=gain_of(PASSES * r).rearrange("p s (h j) -> p s h j", h=HEADS),
                     op=ALU.mult,
                 )
             tiles["folded", r] = folded
 
         def turn(k):
-            turned = stream.tile([P, HEADS, SLOTS, R], F32)
-            if k % PASSES < B:
-                table = tiles["folded", k // PASSES][:]
-            else:
-                table = cos_sin[:, SLOTS : 2 * SLOTS, :].unsqueeze(1).to_broadcast([P, HEADS, SLOTS, R])
-            nc.vector.tensor_tensor(out=turned[:], in0=tiles["g", k][:], in1=table, op=ALU.mult)
+            turned = stream.tile([P, SLOTS, HEADS, R], F32)
+            for i, (s, h, cols) in enumerate(pairs):
+                if k % PASSES < B:
+                    table = tiles["folded", k // PASSES][:, s, h, :]
+                else:
+                    table = cos_sin[:, SLOTS + s, :]
+                nc.vector.scalar_tensor_tensor(
+                    out=turned[:, s, h, :],
+                    in0=tiles["g", k][:, h, s, :],
+                    scalar=tiles["rho", k][:, i : i + 1],
+                    in1=table,
+                    op0=ALU.mult,
+                    op1=ALU.mult,
+                )
             tiles["turned", k] = turned
 
         def add_halves(k):
             dv = stream.tile([P, SLOTS, CHUNK], F32)
             turned = tiles["turned", k]
             nc.vector.tensor_tensor(
-                out=dv[:].rearrange("p s (h j) -> p h s j", h=HEADS),
+                out=dv[:].rearrange("p s (h j) -> p s h j", h=HEADS),
                 in0=turned[:, :, :, 0:DH],
                 in1=turned[:, :, :, DH:R],
                 op=ALU.add,
@@ -240,14 +238,6 @@ def tile_cmattention_pa_v_kernel(tc, x, a, Wq_x, Wq_a, qx_scale, qa_scale, p_x, 
             nc.vector.tensor_tensor(out=prod[:], in0=tiles["p", k][:], in1=tiles["dv", k][:], op=ALU.mult)
             tiles["prod", k] = prod
 
-        def scale_dv(k):
-            scaled = stream.tile([P, SLOTS, CHUNK], F32)
-            for i, (s, h, cols) in enumerate(pairs):
-                nc.scalar.activation(
-                    out=scaled[:, s, cols], in_=tiles["dv", k][:, s, cols], func=ACT.Copy, scale=tiles["rho", k][:, i : i + 1]
-                )
-            tiles["scaled", k] = scaled
-
         def project(k):
             back = stream.tile([P, SLOTS * HEADS], F32)
             for i, (s, h, cols) in enumerate(pairs):
@@ -255,7 +245,7 @@ def tile_cmattention_pa_v_kernel(tc, x, a, Wq_x, Wq_a, qx_scale, qa_scale, p_x, 
                     out=tiles["prod", k][:, s, cols],
                     in_=tiles["prod", k][:, s, cols],
                     func=ACT.Copy,
-                    scale=tiles["minus_rho3", k][:, i : i + 1],
+                    scale=tiles["minus_inv", k][:, i : i + 1],
                     accum_out=back[:, i : i + 1],
                 )
             along = stream.tile([P, SLOTS, CHUNK], F32)
@@ -269,7 +259,7 @@ def tile_cmattention_pa_v_kernel(tc, x, a, Wq_x, Wq_a, qx_scale, qa_scale, p_x, 
             dp = stream.tile([P, CHUNK * SLOTS], BF16, align_bytes=64)
             nc.vector.tensor_tensor(
                 out=dp[:].rearrange("p (c i s) -> p c s i", i=RUN, s=SLOTS),
-                in0=tiles["scaled", k][:].rearrange("p s (c i) -> p c s i", i=RUN),
+                in0=tiles["dv", k][:].rearrange("p s (c i) -> p c s i", i=RUN),
                 in1=tiles["along", k][:].rearrange("p s (c i) -> p c s i", i=RUN),
                 op=ALU.add,
             )
@@ -305,11 +295,7 @@ def tile_cmattention_pa_v_kernel(tc, x, a, Wq_x, Wq_a, qx_scale, qa_scale, p_x, 
                 rows = slice(CHUNK * r + P * m, CHUNK * r + P * m + P)
                 result = stream.tile([P, D], F32)
                 for n in range(N_TILES):
-                    n_cols = slice(N_TILE * n, N_TILE * n + N_TILE)
-                    if m == 0:
-                        nc.scalar.copy(out=result[:, n_cols], in_=tiles["sum", r, m, n][:])
-                    else:
-                        nc.vector.tensor_copy(out=result[:, n_cols], in_=tiles["sum", r, m, n][:])
+                    nc.scalar.copy(out=result[:, N_TILE * n : N_TILE * n + N_TILE], in_=tiles["sum", r, m, n][:])
                 nc.sync.dma_start(out=out[rows, :], in_=result[:])
 
         def when_live(stage, k, count):
@@ -322,24 +308,19 @@ def tile_cmattention_pa_v_kernel(tc, x, a, Wq_x, Wq_a, qx_scale, qa_scale, p_x, 
                 when_live(load_x, t // 2 + 1, PASSES)
             when_live(load_g, t + 2, CHUNKS)
 
-            when_live(scale_dv, t - 1, CHUNKS)
             when_live(project, t - 1, CHUNKS)
             when_live(root, t + 1, CHUNKS)
             when_live(sum_squares, t + 4, CHUNKS)
-            if t % 2 == 0:
-                when_live(regroup_x, t, PASSES * N_TILES)
+            when_live(regroup_x, t, PASSES * N_TILES)
 
             when_live(turn, t, CHUNKS)
             when_live(quantise_dp, t - 2, CHUNKS)
             when_live(add_halves, t, CHUNKS)
             when_live(clamp_norm, t + 3, CHUNKS)
             when_live(invert_norm, t + 2, CHUNKS)
-            when_live(cube, t, CHUNKS)
             if t % PASSES == B:
                 when_live(apply_gain, t, CHUNKS)
             when_live(quantise_x, t - 1, PASSES * N_TILES)
-            if t % 2 == 1:
-                when_live(regroup_x, t, PASSES * N_TILES)
             when_live(times_p, t, CHUNKS)
             if (t + 1) % PASSES == 0:
                 when_live(fold_gain, (t + 1) // PASSES, ROUNDS)

@@ -1,5 +1,6 @@
 import math
 
+import concourse.masks as masks
 import concourse.mybir as mybir
 
 FLOPS = 2 * 2560 * 1024 * 1024
@@ -107,7 +108,7 @@ def tile_cmattention_pa_v_kernel(tc, x, a, Wq_x, Wq_a, qx_scale, qa_scale, p_x, 
         tc.tile_pool(name="consts", bufs=1) as consts,
         tc.tile_pool(name="keep", bufs=1) as keep,
         tc.tile_pool(name="stream", bufs=2) as stream,
-        tc.psum_pool(name="psum", bufs=2) as psum,
+        tc.psum_pool(name="psum", bufs=1) as psum,
         tc.manual_schedule(),
     ):
         x_codes = keep.tile([P, PASSES, D], U32, align_bytes=64)
@@ -192,21 +193,36 @@ def tile_cmattention_pa_v_kernel(tc, x, a, Wq_x, Wq_a, qx_scale, qa_scale, p_x, 
             return gain[:, dp_cols(k)].unsqueeze(1).to_broadcast([P, SLOTS, CHUNK])
 
         def fold_gain(r):
-            folded = stream.tile([P, SLOTS, HEADS, R], F32)
+            folded = stream.tile([P, HEADS, SLOTS, R], F32)
             for half in range(2):
                 nc.vector.tensor_tensor(
                     out=folded[:, :, :, DH * half : DH * half + DH],
-                    in0=cos_sin[:, 0:SLOTS, DH * half : DH * half + DH].unsqueeze(2).to_broadcast([P, SLOTS, HEADS, DH]),
-                    in1=gain_of(PASSES * r).rearrange("p s (h j) -> p s h j", h=HEADS),
+                    in0=cos_sin[:, 0:SLOTS, DH * half : DH * half + DH].unsqueeze(1).to_broadcast([P, HEADS, SLOTS, DH]),
+                    in1=gain[:, dp_cols(PASSES * r)]
+                    .rearrange("p (h j) -> p h j", h=HEADS)
+                    .unsqueeze(2)
+                    .to_broadcast([P, HEADS, SLOTS, DH]),
                     op=ALU.mult,
                 )
             tiles["folded", r] = folded
+
+        def table_to_psum(r):
+            for h in range(HEADS):
+                tab = psum.tile([P, SLOTS * R], F32, name="tab_%d" % h)
+                nc.tensor.matmul(
+                    out=tab[:],
+                    lhsT=ident[:],
+                    rhs=tiles["folded", r][:, h].rearrange("p s k -> p (s k)"),
+                    start=True,
+                    stop=True,
+                )
+                tiles["tab", r, h] = tab
 
         def turn(k):
             turned = stream.tile([P, SLOTS, HEADS, R], F32)
             for i, (s, h, cols) in enumerate(pairs):
                 if k % PASSES < B:
-                    table = tiles["folded", k // PASSES][:, s, h, :]
+                    table = tiles["tab", k // PASSES, h][:, R * s : R * s + R]
                 else:
                     table = cos_sin[:, SLOTS + s, :]
                 nc.vector.scalar_tensor_tensor(
@@ -220,7 +236,7 @@ def tile_cmattention_pa_v_kernel(tc, x, a, Wq_x, Wq_a, qx_scale, qa_scale, p_x, 
             tiles["turned", k] = turned
 
         def add_halves(k):
-            dv = stream.tile([P, SLOTS, CHUNK], F32)
+            dv = stream.tile([P, SLOTS, CHUNK], F32, bufs=3)
             turned = tiles["turned", k]
             nc.vector.tensor_tensor(
                 out=dv[:].rearrange("p s (h j) -> p s h j", h=HEADS),
@@ -235,7 +251,16 @@ def tile_cmattention_pa_v_kernel(tc, x, a, Wq_x, Wq_a, qx_scale, qa_scale, p_x, 
 
         def times_p(k):
             prod = stream.tile([P, SLOTS, CHUNK], F32)
-            nc.vector.tensor_tensor(out=prod[:], in0=tiles["p", k][:], in1=tiles["dv", k][:], op=ALU.mult)
+            if (k + 1) % PASSES == B:
+                nc.vector.tensor_tensor(out=prod[:], in0=tiles["p", k][:], in1=tiles["dv", k][:], op=ALU.mult)
+            else:
+                for s0 in range(0, SLOTS, 2):
+                    nc.gpsimd.tensor_tensor(
+                        out=prod[:, s0 : s0 + 2],
+                        in0=tiles["p", k][:, s0 : s0 + 2],
+                        in1=tiles["dv", k][:, s0 : s0 + 2],
+                        op=ALU.mult,
+                    )
             tiles["prod", k] = prod
 
         def project(k):
@@ -302,41 +327,60 @@ def tile_cmattention_pa_v_kernel(tc, x, a, Wq_x, Wq_a, qx_scale, qa_scale, p_x, 
             if 0 <= k < count:
                 stage(k)
 
+        def ready_step(k):
+            r, c = k // PASSES, k % PASSES
+            ready = k + 3
+            if r == 0:
+                ready = max(ready, 2 * c + 2)
+            elif c == 0:
+                ready = max(ready, ready_step(k - 1) + 1)
+            else:
+                ready = max(ready, ready_step(k - 1))
+            return ready
+
         def step(t):
             when_live(load_p, t + 5, CHUNKS)
             if t % 2 == 0:
                 when_live(load_x, t // 2 + 1, PASSES)
             when_live(load_g, t + 2, CHUNKS)
 
-            when_live(project, t - 1, CHUNKS)
-            when_live(root, t + 1, CHUNKS)
+            for r in range(ROUNDS):
+                if ready_step(PASSES * r + PASSES - 1) + 1 == t:
+                    store_round(r)
             when_live(sum_squares, t + 4, CHUNKS)
+            when_live(root, t + 1, CHUNKS)
             when_live(regroup_x, t, PASSES * N_TILES)
+            when_live(project, t - 1, CHUNKS)
+
+            if (t + 1) % PASSES == 0:
+                when_live(table_to_psum, (t + 1) // PASSES, ROUNDS)
 
             when_live(turn, t, CHUNKS)
-            when_live(quantise_dp, t - 2, CHUNKS)
-            when_live(add_halves, t, CHUNKS)
+            when_live(round_dp, t - 2, CHUNKS)
+            if t % PASSES >= B - 1:
+                when_live(add_halves, t, CHUNKS)
+            when_live(quantise_dp, t - 3, CHUNKS)
             when_live(clamp_norm, t + 3, CHUNKS)
             when_live(invert_norm, t + 2, CHUNKS)
+            when_live(quantise_x, t - 1, PASSES * N_TILES)
+            if (t + 2) % PASSES == 0:
+                when_live(fold_gain, (t + 2) // PASSES, ROUNDS)
             if t % PASSES == B:
                 when_live(apply_gain, t, CHUNKS)
-            when_live(quantise_x, t - 1, PASSES * N_TILES)
+            if t % PASSES < B - 1:
+                when_live(add_halves, t, CHUNKS)
             when_live(times_p, t, CHUNKS)
-            if (t + 1) % PASSES == 0:
-                when_live(fold_gain, (t + 1) // PASSES, ROUNDS)
-            when_live(round_dp, t - 1, CHUNKS)
 
-            if t % 2 == 0:
-                when_live(multiply, t // 2 - 1, PASSES)
-            if t - 2 >= PASSES:
-                when_live(multiply, t - 2, CHUNKS)
-            if t % PASSES == 1:
-                when_live(store_round, t // PASSES - 2, ROUNDS)
+            for k in range(CHUNKS):
+                if ready_step(k) == t:
+                    multiply(k)
 
         gain = consts.tile([P, H * DH], BF16)
         step(-5)
         step(-4)
         nc.sync.dma_start(out=gain[:], in_=qx_scale.rearrange("h o j -> (h o j)").partition_broadcast(P))
+        ident = consts.tile([P, P], F32)
+        masks.make_identity(nc, ident[:])
         cos_sin = build_rotary_table(nc, consts)
-        for t in range(-3, PASSES * (ROUNDS + 2) + 2):
+        for t in range(-3, ready_step(CHUNKS - 1) + 2):
             step(t)

@@ -36,70 +36,16 @@ BASE = 10000.0
 ROUND_MAGIC = 1.5 * 2.0**23
 TWO_PI_HI = 6.28125
 TWO_PI_LO = 2.0 * math.pi - TWO_PI_HI
+GROUPS = SLOTS * HEADS
+SUB = 8
+SCALAR_SUMS = (11, 13, 15, 17, 19)
+KINDS = 2
 
 
 def token_rows(c):
     if c < B:
         return [(0, P, c, 0, MAIN_N)]
     return [(REST_P * b, REST_P, b, MAIN_N, N) for b in range(B)]
-
-
-def build_rotary_table(nc, consts):
-    kinds = 2 * SLOTS
-    pos_int = consts.tile([P, 2, SLOTS], I32)
-    nc.gpsimd.iota(pos_int[:, 0, :], pattern=[[1, SLOTS]], base=0, channel_multiplier=SLOTS)
-    nc.vector.tensor_single_scalar(
-        out=pos_int[:, 1, :], in_=pos_int[:, 0, :], scalar=SLOTS * REST_P - 1, op=ALU.bitwise_and
-    )
-    pos = consts.tile([P, 2, SLOTS], F32)
-    nc.vector.tensor_copy(out=pos[:, 0, :], in_=pos_int[:, 0, :])
-    nc.vector.tensor_scalar(
-        out=pos[:, 1, :], in0=pos_int[:, 1, :], scalar1=float(MAIN_N), scalar2=None, op0=ALU.add
-    )
-
-    theta = consts.tile([P, kinds, DH], F32)
-    for j in range(DH):
-        nc.vector.tensor_scalar(
-            out=theta[:, :, j],
-            in0=pos[:].rearrange("p k s -> p (k s)"),
-            scalar1=1.0 / (BASE ** (2 * j / R)),
-            scalar2=None,
-            op0=ALU.mult,
-        )
-
-    turns = consts.tile([P, kinds, DH], F32)
-    nc.vector.tensor_scalar(
-        out=turns[:], in0=theta[:], scalar1=1.0 / (2.0 * math.pi), scalar2=ROUND_MAGIC, op0=ALU.mult, op1=ALU.add
-    )
-    nc.vector.tensor_scalar(out=turns[:], in0=turns[:], scalar1=ROUND_MAGIC, scalar2=None, op0=ALU.subtract)
-    rem = consts.tile([P, kinds, DH], F32)
-    nc.vector.scalar_tensor_tensor(
-        out=rem[:], in0=turns[:], scalar=-TWO_PI_HI, in1=theta[:], op0=ALU.mult, op1=ALU.add
-    )
-    nc.vector.scalar_tensor_tensor(
-        out=rem[:], in0=turns[:], scalar=-TWO_PI_LO, in1=rem[:], op0=ALU.mult, op1=ALU.add
-    )
-
-    sin_half = consts.tile([P, kinds, DH], F32)
-    nc.scalar.activation(out=sin_half[:], in_=rem[:], func=ACT.Sin, scale=0.5)
-    quarter = consts.tile([P, kinds, DH], F32)
-    nc.vector.scalar_tensor_tensor(out=quarter[:], in0=rem[:], scalar=-1.0, in1=rem[:], op0=ALU.mult, op1=ALU.max)
-    nc.vector.tensor_scalar(
-        out=quarter[:], in0=quarter[:], scalar1=-0.5, scalar2=math.pi / 2.0, op0=ALU.mult, op1=ALU.add
-    )
-    cos_half = consts.tile([P, kinds, DH], F32)
-    nc.scalar.activation(out=cos_half[:], in_=quarter[:], func=ACT.Sin)
-
-    cos_sin = consts.tile([P, kinds, R], F32)
-    squared = consts.tile([P, kinds, DH], F32)
-    nc.vector.tensor_tensor(out=squared[:], in0=sin_half[:], in1=sin_half[:], op=ALU.mult)
-    nc.vector.tensor_scalar(
-        out=cos_sin[:, :, 0:DH], in0=squared[:], scalar1=-2.0, scalar2=1.0, op0=ALU.mult, op1=ALU.add
-    )
-    nc.vector.scalar_tensor_tensor(
-        out=cos_sin[:, :, DH:R], in0=sin_half[:], scalar=2.0, in1=cos_half[:], op0=ALU.mult, op1=ALU.mult
-    )
-    return cos_sin
 
 
 def tile_cmattention_pa_v_kernel(tc, x, a, Wq_x, Wq_a, qx_scale, qa_scale, p_x, grad_out, out):
@@ -117,7 +63,7 @@ def tile_cmattention_pa_v_kernel(tc, x, a, Wq_x, Wq_a, qx_scale, qa_scale, p_x, 
         dp_scales = keep.tile([P, PASSES, H * DH], U8, align_bytes=64)
 
         tiles = {}
-        pairs = [(s, h, slice(DH * h, DH * h + DH)) for s in range(SLOTS) for h in range(HEADS)]
+        pairs = [(HEADS * s + h, s, h, slice(DH * h, DH * h + DH)) for h in range(HEADS) for s in range(SLOTS)]
 
         def dp_cols(k):
             return slice(CHUNK * (k // PASSES), CHUNK * (k // PASSES) + CHUNK)
@@ -130,14 +76,17 @@ def tile_cmattention_pa_v_kernel(tc, x, a, Wq_x, Wq_a, qx_scale, qa_scale, p_x, 
                 )
             tiles["x_rows", c] = x_rows
 
-        def regroup_x(i):
+        def regroup_x(i, copy):
             n_cols = slice(N_TILE * (i % N_TILES), N_TILE * (i % N_TILES) + N_TILE)
-            x_grouped = stream.tile([P, N_TILE * SLOTS], BF16, align_bytes=64)
-            nc.scalar.copy(
+            x_grouped = stream.tile([P, N_TILE * SLOTS], BF16, align_bytes=64, bufs=3)
+            copy(
                 out=x_grouped[:].rearrange("p (c i s) -> p c s i", i=RUN, s=SLOTS),
                 in_=tiles["x_rows", i // N_TILES][:, :, n_cols].rearrange("p s (c i) -> p c s i", i=RUN),
             )
             tiles["x_grouped", i] = x_grouped
+
+        def regroup_x_scalar(i):
+            regroup_x(i, nc.scalar.copy)
 
         def quantise_x(i):
             n_cols = slice(N_TILE * (i % N_TILES), N_TILE * (i % N_TILES) + N_TILE)
@@ -148,7 +97,7 @@ def tile_cmattention_pa_v_kernel(tc, x, a, Wq_x, Wq_a, qx_scale, qa_scale, p_x, 
             )
 
         def load_p(k):
-            p = stream.tile([P, SLOTS, CHUNK], F32, bufs=7)
+            p = stream.tile([P, SLOTS, CHUNK], F32, bufs=8)
             for p0, parts, b, n0, n1 in token_rows(k % PASSES):
                 nc.sync.dma_start(
                     out=p[p0 : p0 + parts], in_=p_x[b, n0:n1, dp_cols(k)].rearrange("(p s) k -> p s k", s=SLOTS)
@@ -166,16 +115,15 @@ def tile_cmattention_pa_v_kernel(tc, x, a, Wq_x, Wq_a, qx_scale, qa_scale, p_x, 
             tiles["g", k] = g
 
         def sum_squares(k):
-            norm2 = stream.tile([P, SLOTS * HEADS], F32, bufs=3)
-            squares = stream.tile([P, SLOTS, CHUNK], BF16)
-            for i, (s, h, cols) in enumerate(pairs):
+            norm2 = stream.tile([P, GROUPS], F32, bufs=3)
+            for i, s, h, cols in pairs:
                 nc.scalar.activation(
-                    out=squares[:, s, cols], in_=tiles["p", k][:, s, cols], func=ACT.Square, accum_out=norm2[:, i : i + 1]
+                    out=junk[:], in_=tiles["p", k][:, s, cols], func=ACT.Square, accum_out=norm2[:, i : i + 1]
                 )
             tiles["norm2", k] = norm2
 
         def clamp_norm(k):
-            minus_inv = stream.tile([P, SLOTS * HEADS], F32, bufs=5)
+            minus_inv = stream.tile([P, GROUPS], F32, bufs=6)
             nc.vector.tensor_scalar(
                 out=minus_inv[:], in0=tiles["norm2", k][:], scalar1=EPS * EPS, scalar2=-1.0, op0=ALU.max, op1=ALU.mult
             )
@@ -185,58 +133,48 @@ def tile_cmattention_pa_v_kernel(tc, x, a, Wq_x, Wq_a, qx_scale, qa_scale, p_x, 
             nc.vector.reciprocal(out=tiles["minus_inv", k][:], in_=tiles["minus_inv", k][:])
 
         def root(k):
-            rho = stream.tile([P, SLOTS * HEADS], F32)
+            rho = stream.tile([P, GROUPS], F32)
             nc.scalar.activation(out=rho[:], in_=tiles["minus_inv", k][:], func=ACT.Sqrt, scale=-1.0)
             tiles["rho", k] = rho
 
-        def gain_of(k):
-            return gain[:, dp_cols(k)].unsqueeze(1).to_broadcast([P, SLOTS, CHUNK])
-
-        def fold_gain(r):
-            folded = stream.tile([P, HEADS, SLOTS, R], F32)
-            for half in range(2):
-                nc.vector.tensor_tensor(
-                    out=folded[:, :, :, DH * half : DH * half + DH],
-                    in0=cos_sin[:, 0:SLOTS, DH * half : DH * half + DH].unsqueeze(1).to_broadcast([P, HEADS, SLOTS, DH]),
-                    in1=gain[:, dp_cols(PASSES * r)]
-                    .rearrange("p (h j) -> p h j", h=HEADS)
-                    .unsqueeze(2)
-                    .to_broadcast([P, HEADS, SLOTS, DH]),
-                    op=ALU.mult,
+        def fold_gain(u):
+            r, kind = u // KINDS, u % KINDS
+            folded = stream.tile([P, HEADS, SLOTS * P], F32)
+            for h in range(HEADS):
+                nc.vector.tensor_scalar(
+                    out=folded[:, h, :],
+                    in0=table_t[:, kind, :],
+                    scalar1=gain_t[:, HEADS * r + h : HEADS * r + h + 1],
+                    scalar2=None,
+                    op0=ALU.mult,
                 )
-            tiles["folded", r] = folded
+            tiles["folded", u] = folded
 
-        def table_to_psum(r):
+        def lay_table(u):
             for h in range(HEADS):
                 tab = psum.tile([P, SLOTS * R], F32, name="tab_%d" % h)
-                nc.tensor.matmul(
-                    out=tab[:],
-                    lhsT=ident[:],
-                    rhs=tiles["folded", r][:, h].rearrange("p s k -> p (s k)"),
-                    start=True,
-                    stop=True,
-                )
-                tiles["tab", r, h] = tab
+                for s in range(SLOTS):
+                    nc.tensor.transpose(
+                        out=tab[:, R * s : R * s + R], in_=tiles["folded", u][:, h, P * s : P * s + P], identity=ident[:]
+                    )
+                tiles["tab", u, h] = tab
 
         def turn(k):
+            u = KINDS * (k // PASSES) + (1 if k % PASSES == B else 0)
             turned = stream.tile([P, SLOTS, HEADS, R], F32)
-            for i, (s, h, cols) in enumerate(pairs):
-                if k % PASSES < B:
-                    table = tiles["tab", k // PASSES, h][:, R * s : R * s + R]
-                else:
-                    table = cos_sin[:, SLOTS + s, :]
+            for i, s, h, cols in pairs:
                 nc.vector.scalar_tensor_tensor(
                     out=turned[:, s, h, :],
                     in0=tiles["g", k][:, h, s, :],
                     scalar=tiles["rho", k][:, i : i + 1],
-                    in1=table,
+                    in1=tiles["tab", u, h][:, R * s : R * s + R],
                     op0=ALU.mult,
                     op1=ALU.mult,
                 )
             tiles["turned", k] = turned
 
         def add_halves(k):
-            dv = stream.tile([P, SLOTS, CHUNK], F32, bufs=3)
+            dv = stream.tile([P, SLOTS, CHUNK], F32, bufs=4)
             turned = tiles["turned", k]
             nc.vector.tensor_tensor(
                 out=dv[:].rearrange("p s (h j) -> p s h j", h=HEADS),
@@ -246,12 +184,9 @@ def tile_cmattention_pa_v_kernel(tc, x, a, Wq_x, Wq_a, qx_scale, qa_scale, p_x, 
             )
             tiles["dv", k] = dv
 
-        def apply_gain(k):
-            nc.vector.tensor_tensor(out=tiles["dv", k][:], in0=tiles["dv", k][:], in1=gain_of(k), op=ALU.mult)
-
         def times_p(k):
             prod = stream.tile([P, SLOTS, CHUNK], F32)
-            if (k + 1) % PASSES == B:
+            if k == CHUNKS - 1:
                 nc.vector.tensor_tensor(out=prod[:], in0=tiles["p", k][:], in1=tiles["dv", k][:], op=ALU.mult)
             else:
                 for s0 in range(0, SLOTS, 2):
@@ -263,9 +198,37 @@ def tile_cmattention_pa_v_kernel(tc, x, a, Wq_x, Wq_a, qx_scale, qa_scale, p_x, 
                     )
             tiles["prod", k] = prod
 
-        def project(k):
-            back = stream.tile([P, SLOTS * HEADS], F32)
-            for i, (s, h, cols) in enumerate(pairs):
+        def tensor_sums(k):
+            sums = sums_bank[:, k % 4, :]
+            stretches = tiles["prod", k][:].rearrange("p s (h a b) -> p (s h) a b", a=DH // SUB, b=SUB)
+            for a0 in range(DH // SUB):
+                nc.tensor.matmul(
+                    out=sums.rearrange("p (g b) -> p g b", b=SUB),
+                    lhsT=ident[:],
+                    rhs=stretches[:, :, a0, :],
+                    start=(a0 == 0),
+                    stop=(a0 == DH // SUB - 1),
+                )
+            tiles["sums", k] = sums
+
+        def scale_sums(k):
+            scaled = stream.tile([P, GROUPS, SUB], F32)
+            nc.vector.tensor_tensor(
+                out=scaled[:],
+                in0=tiles["sums", k].rearrange("p (g b) -> p g b", b=SUB),
+                in1=tiles["minus_inv", k][:].unsqueeze(2).to_broadcast([P, GROUPS, SUB]),
+                op=ALU.mult,
+            )
+            tiles["scaled", k] = scaled
+
+        def finish_sums(k):
+            back = stream.tile([P, GROUPS], F32, name="back", bufs=3)
+            nc.vector.tensor_reduce(out=back[:], in_=tiles["scaled", k][:], axis=mybir.AxisListType.X, op=ALU.add)
+            tiles["back", k] = back
+
+        def scalar_sums(k):
+            back = stream.tile([P, GROUPS], F32, name="back", bufs=3)
+            for i, s, h, cols in pairs:
                 nc.scalar.activation(
                     out=tiles["prod", k][:, s, cols],
                     in_=tiles["prod", k][:, s, cols],
@@ -273,10 +236,13 @@ def tile_cmattention_pa_v_kernel(tc, x, a, Wq_x, Wq_a, qx_scale, qa_scale, p_x, 
                     scale=tiles["minus_inv", k][:, i : i + 1],
                     accum_out=back[:, i : i + 1],
                 )
+            tiles["back", k] = back
+
+        def project(k):
             along = stream.tile([P, SLOTS, CHUNK], F32)
-            for i, (s, h, cols) in enumerate(pairs):
+            for i, s, h, cols in pairs:
                 nc.scalar.activation(
-                    out=along[:, s, cols], in_=tiles["p", k][:, s, cols], func=ACT.Copy, scale=back[:, i : i + 1]
+                    out=along[:, s, cols], in_=tiles["p", k][:, s, cols], func=ACT.Copy, scale=tiles["back", k][:, i : i + 1]
                 )
             tiles["along", k] = along
 
@@ -297,90 +263,205 @@ def tile_cmattention_pa_v_kernel(tc, x, a, Wq_x, Wq_a, qx_scale, qa_scale, p_x, 
                 in_=tiles["dp", k][:],
             )
 
-        def multiply(k):
-            r, c = k // PASSES, k % PASSES
-            for m in range(M_TILES):
-                rows = slice(CHUNK * r + P * m, CHUNK * r + P * m + P)
-                for n in range(N_TILES):
-                    if c == 0:
-                        tiles["sum", r, m, n] = psum.tile([P, N_TILE], F32, name="sum_%d_%d" % (m, n))
-                    n_cols = slice(N_TILE * n, N_TILE * n + N_TILE)
-                    nc.tensor.matmul_mx(
-                        out=tiles["sum", r, m, n][:],
-                        lhsT=dp_codes[:, c, rows].bitcast(E5M2X4),
-                        lhsT_scale=dp_scales[:, c, rows],
-                        rhs=x_codes[:, c, n_cols].bitcast(E4M3X4),
-                        rhs_scale=x_scales[:, c, n_cols],
-                        start=(c == 0),
-                        stop=(c == PASSES - 1),
-                    )
+        def mx_pass(q, c, bank):
+            if c == 0:
+                tiles["sum", q] = psum.tile([P, N_TILE], F32, name=bank)
+            row0 = P * (q // N_TILES)
+            n_cols = slice(N_TILE * (q % N_TILES), N_TILE * (q % N_TILES) + N_TILE)
+            nc.tensor.matmul_mx(
+                out=tiles["sum", q][:],
+                lhsT=dp_codes[:, c, row0 : row0 + P].bitcast(E5M2X4),
+                lhsT_scale=dp_scales[:, c, row0 : row0 + P],
+                rhs=x_codes[:, c, n_cols].bitcast(E4M3X4),
+                rhs_scale=x_scales[:, c, n_cols],
+                start=(c == 0),
+                stop=(c == PASSES - 1),
+            )
 
-        def store_round(r):
-            for m in range(M_TILES):
-                rows = slice(CHUNK * r + P * m, CHUNK * r + P * m + P)
-                result = stream.tile([P, D], F32)
-                for n in range(N_TILES):
-                    nc.scalar.copy(out=result[:, N_TILE * n : N_TILE * n + N_TILE], in_=tiles["sum", r, m, n][:])
-                nc.sync.dma_start(out=out[rows, :], in_=result[:])
+        def store_group(q, copy):
+            row0 = P * (q // N_TILES)
+            n_cols = slice(N_TILE * (q % N_TILES), N_TILE * (q % N_TILES) + N_TILE)
+            result = stream.tile([P, N_TILE], F32, bufs=4)
+            copy(out=result[:], in_=tiles["sum", q][:])
+            nc.sync.dma_start(out=out[row0 : row0 + P, n_cols], in_=result[:])
+
+        per_round = M_TILES * N_TILES
+        early = per_round * (ROUNDS - 1)
+
+        def group_step(q):
+            first = PASSES * (q // per_round) + PASSES - 1 + 5
+            return first if q == 0 else max(first, group_step(q - 1) + 1)
 
         def when_live(stage, k, count):
             if 0 <= k < count:
                 stage(k)
 
-        def ready_step(k):
-            r, c = k // PASSES, k % PASSES
-            ready = k + 3
-            if r == 0:
-                ready = max(ready, 2 * c + 2)
-            elif c == 0:
-                ready = max(ready, ready_step(k - 1) + 1)
-            else:
-                ready = max(ready, ready_step(k - 1))
-            return ready
-
         def step(t):
             when_live(load_p, t + 5, CHUNKS)
             if t % 2 == 0:
-                when_live(load_x, t // 2 + 1, PASSES)
+                when_live(load_x, t // 2 + 2, PASSES)
             when_live(load_g, t + 2, CHUNKS)
 
-            for r in range(ROUNDS):
-                if ready_step(PASSES * r + PASSES - 1) + 1 == t:
-                    store_round(r)
-            when_live(sum_squares, t + 4, CHUNKS)
-            when_live(root, t + 1, CHUNKS)
-            when_live(regroup_x, t, PASSES * N_TILES)
-            when_live(project, t - 1, CHUNKS)
+            for q in range(early):
+                if group_step(q) == t:
+                    for c in range(PASSES):
+                        mx_pass(q, c, "acc_%d" % (q % 3))
 
-            if (t + 1) % PASSES == 0:
-                when_live(table_to_psum, (t + 1) // PASSES, ROUNDS)
+            for q in range(early):
+                if group_step(q) + 1 == t:
+                    store_group(q, nc.scalar.copy)
+            when_live(sum_squares, t + 4, CHUNKS)
+            if t > 0:
+                when_live(root, t + 1, CHUNKS)
+            when_live(regroup_x_scalar, t + 2, PASSES * N_TILES)
+            when_live(project, t - 2, CHUNKS) if t - 2 in SCALAR_SUMS else None
 
             when_live(turn, t, CHUNKS)
-            when_live(round_dp, t - 2, CHUNKS)
+            if t - 2 not in SCALAR_SUMS:
+                when_live(scale_sums, t - 2, CHUNKS)
+
             if t % PASSES >= B - 1:
-                when_live(add_halves, t, CHUNKS)
-            when_live(quantise_dp, t - 3, CHUNKS)
+                when_live(lay_table, KINDS * (t // PASSES) + t % PASSES - B + 2, KINDS * ROUNDS)
+            if t - 1 not in SCALAR_SUMS:
+                when_live(tensor_sums, t - 1, CHUNKS)
+
+            when_live(round_dp, t - 3, CHUNKS)
+            if t - 2 not in SCALAR_SUMS:
+                when_live(finish_sums, t - 2, CHUNKS)
+                when_live(project, t - 2, CHUNKS)
+            if t - 1 in SCALAR_SUMS:
+                scalar_sums(t - 1)
+            when_live(quantise_dp, t - 4, CHUNKS)
+            if t == 0:
+                clamp_norm(1)
+                clamp_norm(2)
+            when_live(quantise_x, t + 1, PASSES * N_TILES) if t + 1 >= 2 else None
             when_live(clamp_norm, t + 3, CHUNKS)
+            if t == 0:
+                invert_norm(1)
             when_live(invert_norm, t + 2, CHUNKS)
-            when_live(quantise_x, t - 1, PASSES * N_TILES)
-            if (t + 2) % PASSES == 0:
-                when_live(fold_gain, (t + 2) // PASSES, ROUNDS)
-            if t % PASSES == B:
-                when_live(apply_gain, t, CHUNKS)
-            if t % PASSES < B - 1:
-                when_live(add_halves, t, CHUNKS)
+            if t == 0:
+                root(1)
+            if B - 2 <= t % PASSES < B:
+                when_live(fold_gain, KINDS * (t // PASSES) + t % PASSES - B + 3, KINDS * ROUNDS)
+            when_live(add_halves, t, CHUNKS)
             when_live(times_p, t, CHUNKS)
 
-            for k in range(CHUNKS):
-                if ready_step(k) == t:
-                    multiply(k)
+            c = t - 4 - PASSES * (ROUNDS - 1)
+            if 0 <= c < PASSES:
+                for q in range(early, early + per_round):
+                    mx_pass(q, c, "tab_%d" % (q - early))
 
-        gain = consts.tile([P, H * DH], BF16)
-        step(-5)
-        step(-4)
-        nc.sync.dma_start(out=gain[:], in_=qx_scale.rearrange("h o j -> (h o j)").partition_broadcast(P))
+        sums_bank = psum.tile([P, 4, GROUPS * SUB], F32)
+        junk = consts.tile([P, DH], BF16)
+        warm = consts.tile([P, 2], F32)
+        nc.vector.memset(warm[:, 0:1], 0.0)
+        nc.scalar.activation(out=warm[:, 1:2], in_=warm[:, 0:1], func=ACT.Sin)
+        gain_rows = consts.tile([P, R], BF16)
+        nc.vector.memset(gain_rows[:], 0.0)
+        for half in range(2):
+            nc.sync.dma_start(
+                out=gain_rows[0:H, DH * half : DH * half + DH], in_=qx_scale.rearrange("h o j -> h (o j)")
+            )
+        load_x(0)
+        load_p(0)
+        load_g(0)
+        load_p(1)
+        load_x(1)
+        load_p(2)
+        load_g(1)
+        load_p(3)
+        load_p(4)
         ident = consts.tile([P, P], F32)
         masks.make_identity(nc, ident[:])
-        cos_sin = build_rotary_table(nc, consts)
-        for t in range(-3, ready_step(CHUNKS - 1) + 2):
+
+        kinds = KINDS * SLOTS
+        pos_int = consts.tile([P, KINDS, SLOTS], I32)
+        nc.gpsimd.iota(pos_int[:, 0, :], pattern=[[1, SLOTS]], base=0, channel_multiplier=SLOTS)
+        nc.vector.tensor_single_scalar(
+            out=pos_int[:, 1, :], in_=pos_int[:, 0, :], scalar=SLOTS * REST_P - 1, op=ALU.bitwise_and
+        )
+        pos = consts.tile([P, KINDS, SLOTS], F32)
+        nc.vector.tensor_copy(out=pos[:, 0, :], in_=pos_int[:, 0, :])
+        nc.vector.tensor_scalar(
+            out=pos[:, 1, :], in0=pos_int[:, 1, :], scalar1=float(MAIN_N), scalar2=None, op0=ALU.add
+        )
+        theta = consts.tile([P, kinds, DH], F32)
+        for j in range(DH):
+            if j % 2 == 0:
+                nc.vector.tensor_scalar(
+                    out=theta[:, :, j],
+                    in0=pos[:].rearrange("p k s -> p (k s)"),
+                    scalar1=1.0 / (BASE ** (2 * j / R)),
+                    scalar2=None,
+                    op0=ALU.mult,
+                )
+            else:
+                nc.scalar.activation(
+                    out=theta[:, :, j],
+                    in_=pos[:].rearrange("p k s -> p (k s)"),
+                    func=ACT.Copy,
+                    scale=1.0 / (BASE ** (2 * j / R)),
+                )
+        sum_squares(0)
+        turns = consts.tile([P, kinds, DH], F32)
+        nc.vector.tensor_scalar(
+            out=turns[:], in0=theta[:], scalar1=1.0 / (2.0 * math.pi), scalar2=ROUND_MAGIC, op0=ALU.mult, op1=ALU.add
+        )
+        gain_f32 = consts.tile([P, R], F32)
+        nc.vector.tensor_copy(out=gain_f32[:], in_=gain_rows[:])
+        nc.vector.tensor_scalar(out=turns[:], in0=turns[:], scalar1=ROUND_MAGIC, scalar2=None, op0=ALU.subtract)
+        rem = consts.tile([P, kinds, DH], F32)
+        nc.vector.scalar_tensor_tensor(
+            out=rem[:], in0=turns[:], scalar=-TWO_PI_HI, in1=theta[:], op0=ALU.mult, op1=ALU.add
+        )
+        nc.vector.scalar_tensor_tensor(
+            out=rem[:], in0=turns[:], scalar=-TWO_PI_LO, in1=rem[:], op0=ALU.mult, op1=ALU.add
+        )
+        sin_half = consts.tile([P, kinds, DH], F32)
+        nc.scalar.activation(out=sin_half[:], in_=rem[:], func=ACT.Sin, scale=0.5)
+        quarter = turns
+        nc.vector.scalar_tensor_tensor(out=quarter[:], in0=rem[:], scalar=-1.0, in1=rem[:], op0=ALU.mult, op1=ALU.max)
+        nc.vector.tensor_scalar(
+            out=quarter[:], in0=quarter[:], scalar1=-0.5, scalar2=math.pi / 2.0, op0=ALU.mult, op1=ALU.add
+        )
+        cos_half = theta
+        nc.scalar.activation(out=cos_half[:], in_=quarter[:], func=ACT.Sin)
+        cos_sin = consts.tile([P, kinds, R], F32)
+        squared = rem
+        nc.vector.tensor_tensor(out=squared[:], in0=sin_half[:], in1=sin_half[:], op=ALU.mult)
+        regroup_x(0, nc.vector.tensor_copy)
+        nc.vector.tensor_scalar(
+            out=cos_sin[:, :, 0:DH], in0=squared[:], scalar1=-2.0, scalar2=1.0, op0=ALU.mult, op1=ALU.add
+        )
+        nc.vector.scalar_tensor_tensor(
+            out=cos_sin[:, :, DH:R], in0=sin_half[:], scalar=2.0, in1=cos_half[:], op0=ALU.mult, op1=ALU.mult
+        )
+
+        table_t = consts.tile([P, KINDS, SLOTS * P], F32)
+        gain_t = consts.tile([P, H], F32)
+        turned_gain = psum.tile([P, P], F32, name="tab_2")
+        nc.tensor.transpose(out=turned_gain[:], in_=gain_f32[:], identity=ident[:])
+        nc.scalar.copy(out=gain_t[:], in_=turned_gain[:, 0:H])
+        for kind in range(KINDS):
+            turned_table = psum.tile([P, SLOTS * P], F32, name="tab_%d" % kind)
+            for s in range(SLOTS):
+                nc.tensor.transpose(
+                    out=turned_table[:, P * s : P * s + P], in_=cos_sin[:, SLOTS * kind + s, :], identity=ident[:]
+                )
+            nc.scalar.copy(out=table_t[:, kind, :], in_=turned_table[:])
+        clamp_norm(0)
+        regroup_x(1, nc.vector.tensor_copy)
+        invert_norm(0)
+        quantise_x(0)
+        root(0)
+        fold_gain(0)
+        lay_table(0)
+        quantise_x(1)
+        sum_squares(1)
+        sum_squares(2)
+        sum_squares(3)
+        for t in range(0, CHUNKS + 5):
             step(t)
+        for q in range(early, early + per_round):
+            store_group(q, nc.scalar.copy if q % 2 == 0 else nc.vector.tensor_copy)

@@ -116,9 +116,10 @@ def tile_cmattention_pa_v_kernel(tc, x, a, Wq_x, Wq_a, qx_scale, qa_scale, p_x, 
 
         def sum_squares(k):
             norm2 = stream.tile([P, GROUPS], F32, bufs=3)
+            squares = stream.tile([P, SLOTS, CHUNK], BF16)
             for i, s, h, cols in pairs:
                 nc.scalar.activation(
-                    out=junk[:], in_=tiles["p", k][:, s, cols], func=ACT.Square, accum_out=norm2[:, i : i + 1]
+                    out=squares[:, s, cols], in_=tiles["p", k][:, s, cols], func=ACT.Square, accum_out=norm2[:, i : i + 1]
                 )
             tiles["norm2", k] = norm2
 
@@ -353,7 +354,6 @@ def tile_cmattention_pa_v_kernel(tc, x, a, Wq_x, Wq_a, qx_scale, qa_scale, p_x, 
                     mx_pass(q, c, "tab_%d" % (q - early))
 
         sums_bank = psum.tile([P, 4, GROUPS * SUB], F32)
-        junk = consts.tile([P, DH], BF16)
         warm = consts.tile([P, 2], F32)
         nc.vector.memset(warm[:, 0:1], 0.0)
         nc.scalar.activation(out=warm[:, 1:2], in_=warm[:, 0:1], func=ACT.Sin)

@@ -142,13 +142,13 @@ def tile_cmattention_pa_v_kernel(tc, x, a, Wq_x, Wq_a, qx_scale, qa_scale, p_x, 
             r, kind = u // KINDS, u % KINDS
             folded = stream.tile([P, HEADS, SLOTS * P], F32)
             for h in range(HEADS):
-                nc.vector.tensor_scalar(
-                    out=folded[:, h, :],
-                    in0=table_t[:, kind, :],
-                    scalar1=gain_t[:, HEADS * r + h : HEADS * r + h + 1],
-                    scalar2=None,
-                    op0=ALU.mult,
-                )
+                gain_h = gain_t[:, HEADS * r + h : HEADS * r + h + 1]
+                if u == 0:
+                    nc.vector.tensor_scalar(
+                        out=folded[:, h, :], in0=table_t[:, kind, :], scalar1=gain_h, scalar2=None, op0=ALU.mult
+                    )
+                else:
+                    nc.scalar.activation(out=folded[:, h, :], in_=table_t[:, kind, :], func=ACT.Copy, scale=gain_h)
             tiles["folded", u] = folded
 
         def lay_table(u):
@@ -287,11 +287,30 @@ def tile_cmattention_pa_v_kernel(tc, x, a, Wq_x, Wq_a, qx_scale, qa_scale, p_x, 
             nc.sync.dma_start(out=out[row0 : row0 + P, n_cols], in_=result[:])
 
         per_round = M_TILES * N_TILES
-        early = per_round * (ROUNDS - 1)
+        free_banks = ["acc_0", "acc_1", "acc_2"]
+        open_groups = []
+        waiting = list(range(per_round * ROUNDS))
+        full = []
 
-        def group_step(q):
-            first = PASSES * (q // per_round) + PASSES - 1 + 5
-            return first if q == 0 else max(first, group_step(q - 1) + 1)
+        def pass_step(q, c):
+            return max(PASSES * (q // per_round) + c + 4, 2 * c)
+
+        def empty_banks():
+            for q, bank in full:
+                store_group(q, nc.scalar.copy)
+                free_banks.append(bank)
+            full.clear()
+
+        def multiply(last_step):
+            while free_banks and waiting:
+                open_groups.append([waiting.pop(0), free_banks.pop(0), 0])
+            for group in list(open_groups):
+                while group[2] < PASSES and pass_step(group[0], group[2]) <= last_step:
+                    mx_pass(group[0], group[2], group[1])
+                    group[2] += 1
+                if group[2] == PASSES:
+                    full.append([group[0], group[1]])
+                    open_groups.remove(group)
 
         def when_live(stage, k, count):
             if 0 <= k < count:
@@ -303,17 +322,14 @@ def tile_cmattention_pa_v_kernel(tc, x, a, Wq_x, Wq_a, qx_scale, qa_scale, p_x, 
                 when_live(load_x, t // 2 + 2, PASSES)
             when_live(load_g, t + 2, CHUNKS)
 
-            for q in range(early):
-                if group_step(q) == t:
-                    for c in range(PASSES):
-                        mx_pass(q, c, "acc_%d" % (q % 3))
-
-            for q in range(early):
-                if group_step(q) + 1 == t:
-                    store_group(q, nc.scalar.copy)
-            when_live(sum_squares, t + 4, CHUNKS)
             if t > 0:
                 when_live(root, t + 1, CHUNKS)
+            empty_banks()
+            if t == CHUNKS:
+                free_banks.extend(["tab_%d" % h for h in range(HEADS)])
+            multiply(t - 1)
+
+            when_live(sum_squares, t + 3, CHUNKS)
             when_live(regroup_x_scalar, t + 2, PASSES * N_TILES)
             when_live(project, t - 2, CHUNKS) if t - 2 in SCALAR_SUMS else None
 
@@ -326,32 +342,23 @@ def tile_cmattention_pa_v_kernel(tc, x, a, Wq_x, Wq_a, qx_scale, qa_scale, p_x, 
             if t - 1 not in SCALAR_SUMS:
                 when_live(tensor_sums, t - 1, CHUNKS)
 
+            when_live(quantise_dp, t - 4, CHUNKS)
             when_live(round_dp, t - 3, CHUNKS)
+            if t - 1 in SCALAR_SUMS:
+                scalar_sums(t - 1)
             if t - 2 not in SCALAR_SUMS:
                 when_live(finish_sums, t - 2, CHUNKS)
                 when_live(project, t - 2, CHUNKS)
-            if t - 1 in SCALAR_SUMS:
-                scalar_sums(t - 1)
-            when_live(quantise_dp, t - 4, CHUNKS)
-            if t == 0:
-                clamp_norm(1)
-                clamp_norm(2)
+            when_live(clamp_norm, t + 2, CHUNKS)
             when_live(quantise_x, t + 1, PASSES * N_TILES) if t + 1 >= 2 else None
-            when_live(clamp_norm, t + 3, CHUNKS)
-            if t == 0:
-                invert_norm(1)
             when_live(invert_norm, t + 2, CHUNKS)
-            if t == 0:
-                root(1)
             if B - 2 <= t % PASSES < B:
                 when_live(fold_gain, KINDS * (t // PASSES) + t % PASSES - B + 3, KINDS * ROUNDS)
             when_live(add_halves, t, CHUNKS)
             when_live(times_p, t, CHUNKS)
 
-            c = t - 4 - PASSES * (ROUNDS - 1)
-            if 0 <= c < PASSES:
-                for q in range(early, early + per_round):
-                    mx_pass(q, c, "tab_%d" % (q - early))
+            if t >= CHUNKS:
+                multiply(t)
 
         sums_bank = psum.tile([P, 4, GROUPS * SUB], F32)
         warm = consts.tile([P, 2], F32)
@@ -363,8 +370,8 @@ def tile_cmattention_pa_v_kernel(tc, x, a, Wq_x, Wq_a, qx_scale, qa_scale, p_x, 
             nc.sync.dma_start(
                 out=gain_rows[0:H, DH * half : DH * half + DH], in_=qx_scale.rearrange("h o j -> h (o j)")
             )
-        load_x(0)
         load_p(0)
+        load_x(0)
         load_g(0)
         load_p(1)
         load_x(1)
@@ -422,15 +429,17 @@ def tile_cmattention_pa_v_kernel(tc, x, a, Wq_x, Wq_a, qx_scale, qa_scale, p_x, 
         nc.scalar.activation(out=sin_half[:], in_=rem[:], func=ACT.Sin, scale=0.5)
         quarter = turns
         nc.vector.scalar_tensor_tensor(out=quarter[:], in0=rem[:], scalar=-1.0, in1=rem[:], op0=ALU.mult, op1=ALU.max)
+        clamp_norm(0)
         nc.vector.tensor_scalar(
             out=quarter[:], in0=quarter[:], scalar1=-0.5, scalar2=math.pi / 2.0, op0=ALU.mult, op1=ALU.add
         )
+        invert_norm(0)
         cos_half = theta
         nc.scalar.activation(out=cos_half[:], in_=quarter[:], func=ACT.Sin)
+        root(0)
         cos_sin = consts.tile([P, kinds, R], F32)
         squared = rem
         nc.vector.tensor_tensor(out=squared[:], in0=sin_half[:], in1=sin_half[:], op=ALU.mult)
-        regroup_x(0, nc.vector.tensor_copy)
         nc.vector.tensor_scalar(
             out=cos_sin[:, :, 0:DH], in0=squared[:], scalar1=-2.0, scalar2=1.0, op0=ALU.mult, op1=ALU.add
         )
@@ -450,18 +459,19 @@ def tile_cmattention_pa_v_kernel(tc, x, a, Wq_x, Wq_a, qx_scale, qa_scale, p_x, 
                     out=turned_table[:, P * s : P * s + P], in_=cos_sin[:, SLOTS * kind + s, :], identity=ident[:]
                 )
             nc.scalar.copy(out=table_t[:, kind, :], in_=turned_table[:])
-        clamp_norm(0)
+            if kind == 0:
+                sum_squares(1)
+        sum_squares(2)
+        regroup_x(0, nc.vector.tensor_copy)
         regroup_x(1, nc.vector.tensor_copy)
-        invert_norm(0)
-        quantise_x(0)
-        root(0)
         fold_gain(0)
         lay_table(0)
+        quantise_x(0)
+        clamp_norm(1)
         quantise_x(1)
-        sum_squares(1)
-        sum_squares(2)
-        sum_squares(3)
-        for t in range(0, CHUNKS + 5):
+        invert_norm(1)
+        root(1)
+        for t in range(0, CHUNKS + 4):
             step(t)
-        for q in range(early, early + per_round):
+        for q, bank in full:
             store_group(q, nc.scalar.copy if q % 2 == 0 else nc.vector.tensor_copy)

@@ -190,13 +190,7 @@ def tile_cmattention_pa_v_kernel(tc, x, a, Wq_x, Wq_a, qx_scale, qa_scale, p_x, 
             if k == CHUNKS - 1:
                 nc.vector.tensor_tensor(out=prod[:], in0=tiles["p", k][:], in1=tiles["dv", k][:], op=ALU.mult)
             else:
-                for s0 in range(0, SLOTS, 2):
-                    nc.gpsimd.tensor_tensor(
-                        out=prod[:, s0 : s0 + 2],
-                        in0=tiles["p", k][:, s0 : s0 + 2],
-                        in1=tiles["dv", k][:, s0 : s0 + 2],
-                        op=ALU.mult,
-                    )
+                nc.gpsimd.tensor_tensor(out=prod[:], in0=tiles["p", k][:], in1=tiles["dv", k][:], op=ALU.mult)
             tiles["prod", k] = prod
 
         def tensor_sums(k):
@@ -343,13 +337,13 @@ def tile_cmattention_pa_v_kernel(tc, x, a, Wq_x, Wq_a, qx_scale, qa_scale, p_x, 
                 when_live(tensor_sums, t - 1, CHUNKS)
 
             when_live(quantise_dp, t - 4, CHUNKS)
+            when_live(clamp_norm, t + 2, CHUNKS)
             when_live(round_dp, t - 3, CHUNKS)
             if t - 1 in SCALAR_SUMS:
                 scalar_sums(t - 1)
             if t - 2 not in SCALAR_SUMS:
                 when_live(finish_sums, t - 2, CHUNKS)
                 when_live(project, t - 2, CHUNKS)
-            when_live(clamp_norm, t + 2, CHUNKS)
             when_live(quantise_x, t + 1, PASSES * N_TILES) if t + 1 >= 2 else None
             when_live(invert_norm, t + 2, CHUNKS)
             if B - 2 <= t % PASSES < B:

@@ -36,6 +36,7 @@ BASE = 10000.0
 ROUND_MAGIC = 1.5 * 2.0**23
 TWO_PI_HI = 6.28125
 TWO_PI_LO = 2.0 * math.pi - TWO_PI_HI
+PI_INSIDE = 3.1415925
 GROUPS = SLOTS * HEADS
 SUB = 8
 SCALAR_SUMS = (11, 13, 15, 17, 19)
@@ -345,11 +346,11 @@ def tile_cmattention_pa_v_kernel(tc, x, a, Wq_x, Wq_a, qx_scale, qa_scale, p_x, 
                 when_live(finish_sums, t - 2, CHUNKS)
                 when_live(project, t - 2, CHUNKS)
             when_live(quantise_x, t + 1, PASSES * N_TILES) if t + 1 >= 2 else None
-            when_live(invert_norm, t + 2, CHUNKS)
             if B - 2 <= t % PASSES < B:
                 when_live(fold_gain, KINDS * (t // PASSES) + t % PASSES - B + 3, KINDS * ROUNDS)
             when_live(add_halves, t, CHUNKS)
             when_live(times_p, t, CHUNKS)
+            when_live(invert_norm, t + 2, CHUNKS)
 
             if t >= CHUNKS:
                 multiply(t)
@@ -419,27 +420,20 @@ def tile_cmattention_pa_v_kernel(tc, x, a, Wq_x, Wq_a, qx_scale, qa_scale, p_x, 
         nc.vector.scalar_tensor_tensor(
             out=rem[:], in0=turns[:], scalar=-TWO_PI_LO, in1=rem[:], op0=ALU.mult, op1=ALU.add
         )
-        sin_half = consts.tile([P, kinds, DH], F32)
-        nc.scalar.activation(out=sin_half[:], in_=rem[:], func=ACT.Sin, scale=0.5)
+        nc.vector.tensor_scalar(out=rem[:], in0=rem[:], scalar1=-PI_INSIDE, scalar2=PI_INSIDE, op0=ALU.max, op1=ALU.min)
+        clamp_norm(0)
         quarter = turns
         nc.vector.scalar_tensor_tensor(out=quarter[:], in0=rem[:], scalar=-1.0, in1=rem[:], op0=ALU.mult, op1=ALU.max)
-        clamp_norm(0)
-        nc.vector.tensor_scalar(
-            out=quarter[:], in0=quarter[:], scalar1=-0.5, scalar2=math.pi / 2.0, op0=ALU.mult, op1=ALU.add
-        )
         invert_norm(0)
-        cos_half = theta
-        nc.scalar.activation(out=cos_half[:], in_=quarter[:], func=ACT.Sin)
-        root(0)
-        cos_sin = consts.tile([P, kinds, R], F32)
-        squared = rem
-        nc.vector.tensor_tensor(out=squared[:], in0=sin_half[:], in1=sin_half[:], op=ALU.mult)
         nc.vector.tensor_scalar(
-            out=cos_sin[:, :, 0:DH], in0=squared[:], scalar1=-2.0, scalar2=1.0, op0=ALU.mult, op1=ALU.add
+            out=quarter[:], in0=quarter[:], scalar1=-1.0, scalar2=math.pi / 2.0, op0=ALU.mult, op1=ALU.add
         )
-        nc.vector.scalar_tensor_tensor(
-            out=cos_sin[:, :, DH:R], in0=sin_half[:], scalar=2.0, in1=cos_half[:], op0=ALU.mult, op1=ALU.mult
-        )
+        cos_sin = consts.tile([P, kinds, R], F32)
+        for kind in range(KINDS):
+            of_kind = slice(SLOTS * kind, SLOTS * kind + SLOTS)
+            nc.scalar.activation(out=cos_sin[:, of_kind, DH:R], in_=rem[:, of_kind, :], func=ACT.Sin)
+            nc.scalar.activation(out=cos_sin[:, of_kind, 0:DH], in_=quarter[:, of_kind, :], func=ACT.Sin)
+        root(0)
 
         table_t = consts.tile([P, KINDS, SLOTS * P], F32)
         gain_t = consts.tile([P, H], F32)

@@ -81,8 +81,8 @@ def tile_cmattention_pa_v_kernel(tc, x, a, Wq_x, Wq_a, qx_scale, qa_scale, p_x, 
             n_cols = slice(N_TILE * (i % N_TILES), N_TILE * (i % N_TILES) + N_TILE)
             x_grouped = stream.tile([P, N_TILE * SLOTS], BF16, align_bytes=64, bufs=3)
             copy(
-                out=x_grouped[:].rearrange("p (c i s) -> p c s i", i=RUN, s=SLOTS),
-                in_=tiles["x_rows", i // N_TILES][:, :, n_cols].rearrange("p s (c i) -> p c s i", i=RUN),
+                out=x_grouped[:].rearrange("p (c i s) -> p c s i", i=2 * RUN, s=SLOTS),
+                in_=tiles["x_rows", i // N_TILES][:, :, n_cols].rearrange("p s (c i) -> p c s i", i=2 * RUN),
             )
             tiles["x_grouped", i] = x_grouped
 

@@ -245,9 +245,9 @@ def tile_cmattention_pa_v_kernel(tc, x, a, Wq_x, Wq_a, qx_scale, qa_scale, p_x, 
         def round_dp(k):
             dp = stream.tile([P, CHUNK * SLOTS], BF16, align_bytes=64)
             nc.vector.tensor_tensor(
-                out=dp[:].rearrange("p (c i s) -> p c s i", i=RUN, s=SLOTS),
-                in0=tiles["dv", k][:].rearrange("p s (c i) -> p c s i", i=RUN),
-                in1=tiles["along", k][:].rearrange("p s (c i) -> p c s i", i=RUN),
+                out=dp[:].rearrange("p (c i s) -> p c s i", i=2 * RUN, s=SLOTS),
+                in0=tiles["dv", k][:].rearrange("p s (c i) -> p c s i", i=2 * RUN),
+                in1=tiles["along", k][:].rearrange("p s (c i) -> p c s i", i=2 * RUN),
                 op=ALU.add,
             )
             tiles["dp", k] = dp

@@ -39,7 +39,7 @@ TWO_PI_LO = 2.0 * math.pi - TWO_PI_HI
 PI_INSIDE = 3.1415925
 GROUPS = SLOTS * HEADS
 SUB = 8
-SCALAR_SUMS = (11, 13, 15, 17, 19)
+TURNED_SUMS = (11, 13, 15, 17, 19)
 KINDS = 2
 
 
@@ -188,10 +188,16 @@ def tile_cmattention_pa_v_kernel(tc, x, a, Wq_x, Wq_a, qx_scale, qa_scale, p_x, 
 
         def times_p(k):
             prod = stream.tile([P, SLOTS, CHUNK], F32)
-            if k == CHUNKS - 1:
-                nc.vector.tensor_tensor(out=prod[:], in0=tiles["p", k][:], in1=tiles["dv", k][:], op=ALU.mult)
+            engine = nc.vector if k == CHUNKS - 1 else nc.gpsimd
+            if k in TURNED_SUMS:
+                engine.tensor_tensor(
+                    out=prod[:].rearrange("p s c -> p (s c)").rearrange("p (b g a) -> p g b a", b=DH // SUB, a=SUB),
+                    in0=tiles["p", k][:].rearrange("p s (h b a) -> p (s h) b a", h=HEADS, a=SUB),
+                    in1=tiles["dv", k][:].rearrange("p s (h b a) -> p (s h) b a", h=HEADS, a=SUB),
+                    op=ALU.mult,
+                )
             else:
-                nc.gpsimd.tensor_tensor(out=prod[:], in0=tiles["p", k][:], in1=tiles["dv", k][:], op=ALU.mult)
+                engine.tensor_tensor(out=prod[:], in0=tiles["p", k][:], in1=tiles["dv", k][:], op=ALU.mult)
             tiles["prod", k] = prod
 
         def tensor_sums(k):
@@ -208,30 +214,43 @@ def tile_cmattention_pa_v_kernel(tc, x, a, Wq_x, Wq_a, qx_scale, qa_scale, p_x, 
             tiles["sums", k] = sums
 
         def scale_sums(k):
-            scaled = stream.tile([P, GROUPS, SUB], F32)
-            nc.vector.tensor_tensor(
-                out=scaled[:],
-                in0=tiles["sums", k].rearrange("p (g b) -> p g b", b=SUB),
-                in1=tiles["minus_inv", k][:].unsqueeze(2).to_broadcast([P, GROUPS, SUB]),
-                op=ALU.mult,
+            whole = stream.tile([P, GROUPS], F32, bufs=3)
+            nc.vector.tensor_reduce(
+                out=whole[:], in_=tiles["sums", k].rearrange("p (g b) -> p g b", b=SUB), axis=mybir.AxisListType.X, op=ALU.add
             )
-            tiles["scaled", k] = scaled
+            tiles["whole", k] = whole
 
         def finish_sums(k):
             back = stream.tile([P, GROUPS], F32, name="back", bufs=3)
-            nc.vector.tensor_reduce(out=back[:], in_=tiles["scaled", k][:], axis=mybir.AxisListType.X, op=ALU.add)
+            nc.vector.tensor_tensor(out=back[:], in0=tiles["whole", k][:], in1=tiles["minus_inv", k][:], op=ALU.mult)
             tiles["back", k] = back
 
-        def scalar_sums(k):
-            back = stream.tile([P, GROUPS], F32, name="back", bufs=3)
-            for i, s, h, cols in pairs:
-                nc.scalar.activation(
-                    out=tiles["prod", k][:, s, cols],
-                    in_=tiles["prod", k][:, s, cols],
-                    func=ACT.Copy,
-                    scale=tiles["minus_inv", k][:, i : i + 1],
-                    accum_out=back[:, i : i + 1],
+        def turned_sums(k):
+            sums_t = sums_bank[:, k % 4, :]
+            flat = tiles["prod", k][:].rearrange("p s c -> p (s c)")
+            for b0 in range(DH // SUB):
+                nc.tensor.matmul(
+                    out=sums_t,
+                    lhsT=flat[:, P * b0 : P * b0 + P],
+                    rhs=ident[:],
+                    is_transpose=True,
+                    start=(b0 == 0),
+                    stop=(b0 == DH // SUB - 1),
                 )
+
+        def copy_sums(k):
+            sums_sb = stream.tile([P, P], F32)
+            nc.scalar.copy(out=sums_sb[:], in_=sums_bank[:, k % 4, :])
+            tiles["sums_sb", k] = sums_sb
+
+        def select_sums(k):
+            nc.tensor.matmul(out=sums_bank[:, k % 4, 0:GROUPS], lhsT=tiles["sums_sb", k][:], rhs=sel[:], start=True, stop=True)
+
+        def finish_turned(k):
+            back = stream.tile([P, GROUPS], F32, name="back", bufs=3)
+            nc.vector.tensor_tensor(
+                out=back[:], in0=tiles["minus_inv", k][:], in1=sums_bank[:, k % 4, 0:GROUPS], op=ALU.mult
+            )
             tiles["back", k] = back
 
         def project(k):
@@ -320,34 +339,39 @@ def tile_cmattention_pa_v_kernel(tc, x, a, Wq_x, Wq_a, qx_scale, qa_scale, p_x, 
             if t > 0:
                 when_live(root, t + 1, CHUNKS)
             empty_banks()
+            if t - 2 in TURNED_SUMS:
+                select_sums(t - 2)
             if t == CHUNKS:
                 free_banks.extend(["tab_%d" % h for h in range(HEADS)])
             multiply(t - 1)
 
             when_live(sum_squares, t + 3, CHUNKS)
             when_live(regroup_x_scalar, t + 2, PASSES * N_TILES)
-            when_live(project, t - 2, CHUNKS) if t - 2 in SCALAR_SUMS else None
 
             when_live(turn, t, CHUNKS)
-            if t - 2 not in SCALAR_SUMS:
+            if t - 2 in TURNED_SUMS:
+                finish_turned(t - 2)
+            else:
                 when_live(scale_sums, t - 2, CHUNKS)
 
             if t % PASSES >= B - 1:
                 when_live(lay_table, KINDS * (t // PASSES) + t % PASSES - B + 2, KINDS * ROUNDS)
-            if t - 1 not in SCALAR_SUMS:
+            if t - 1 in TURNED_SUMS:
+                turned_sums(t - 1)
+            else:
                 when_live(tensor_sums, t - 1, CHUNKS)
 
             when_live(quantise_dp, t - 4, CHUNKS)
             when_live(clamp_norm, t + 2, CHUNKS)
             when_live(round_dp, t - 3, CHUNKS)
-            if t - 1 in SCALAR_SUMS:
-                scalar_sums(t - 1)
-            if t - 2 not in SCALAR_SUMS:
+            if t - 2 not in TURNED_SUMS:
                 when_live(finish_sums, t - 2, CHUNKS)
-                when_live(project, t - 2, CHUNKS)
+            when_live(project, t - 2, CHUNKS)
             when_live(quantise_x, t + 1, PASSES * N_TILES) if t + 1 >= 2 else None
             if B - 2 <= t % PASSES < B:
                 when_live(fold_gain, KINDS * (t // PASSES) + t % PASSES - B + 3, KINDS * ROUNDS)
+            if t - 1 in TURNED_SUMS:
+                copy_sums(t - 1)
             when_live(add_halves, t, CHUNKS)
             when_live(times_p, t, CHUNKS)
             when_live(invert_norm, t + 2, CHUNKS)
@@ -374,12 +398,11 @@ def tile_cmattention_pa_v_kernel(tc, x, a, Wq_x, Wq_a, qx_scale, qa_scale, p_x, 
         load_g(1)
         load_p(3)
         load_p(4)
-        ident = consts.tile([P, P], F32)
-        masks.make_identity(nc, ident[:])
-
         kinds = KINDS * SLOTS
         pos_int = consts.tile([P, KINDS, SLOTS], I32)
         nc.gpsimd.iota(pos_int[:, 0, :], pattern=[[1, SLOTS]], base=0, channel_multiplier=SLOTS)
+        ident = consts.tile([P, P], F32)
+        masks.make_identity(nc, ident[:])
         nc.vector.tensor_single_scalar(
             out=pos_int[:, 1, :], in_=pos_int[:, 0, :], scalar=SLOTS * REST_P - 1, op=ALU.bitwise_and
         )
@@ -459,6 +482,10 @@ def tile_cmattention_pa_v_kernel(tc, x, a, Wq_x, Wq_a, qx_scale, qa_scale, p_x, 
         quantise_x(1)
         invert_norm(1)
         root(1)
+        sel = consts.tile([P, GROUPS], F32)
+        nc.vector.tensor_reduce(
+            out=sel[:], in_=ident[:].rearrange("p (g b) -> p g b", b=SUB), axis=mybir.AxisListType.X, op=ALU.add
+        )
         for t in range(0, CHUNKS + 4):
             step(t)
         for q, bank in full:

import math

import concourse.masks as masks
import concourse.mybir as mybir

FLOPS = 2 * 2560 * 1024 * 1024
BYTES = 2560 * 1024 * 2 + 2560 * 1024 * 4 + 2560 * 16 * 128 * 2 + 1024 * 2 + 1024 * 1024 * 4

F32 = mybir.dt.float32
BF16 = mybir.dt.bfloat16
I32 = mybir.dt.int32
U32 = mybir.dt.uint32
U8 = mybir.dt.uint8
E4M3X4 = mybir.dt.float8_e4m3fn_x4
E5M2X4 = mybir.dt.float8_e5m2_x4
ALU = mybir.AluOpType
ACT = mybir.ActivationFunctionType

P = 128
SLOTS = 4
B, N, D, H, DH = 4, 640, 1024, 16, 64
R = 2 * DH
MAIN_N = P * SLOTS
REST_P = (N - MAIN_N) // SLOTS
PASSES = B + 1
HEADS = 4
CHUNK = HEADS * DH
ROUNDS = H // HEADS
CHUNKS = ROUNDS * PASSES
M_TILES = CHUNK // P
N_TILE = 512
N_TILES = D // N_TILE
RUN = 4
EPS = 1e-12
BASE = 10000.0
ROUND_MAGIC = 1.5 * 2.0**23
TWO_PI_HI = 6.28125
TWO_PI_LO = 2.0 * math.pi - TWO_PI_HI
PI_INSIDE = 3.1415925
GROUPS = SLOTS * HEADS
SUB = 8
TURNED_SUMS = (11, 13, 15, 17, 19)
KINDS = 2


def token_rows(c):
    if c < B:
        return [(0, P, c, 0, MAIN_N)]
    return [(REST_P * b, REST_P, b, MAIN_N, N) for b in range(B)]


def tile_cmattention_pa_v_kernel(tc, x, a, Wq_x, Wq_a, qx_scale, qa_scale, p_x, grad_out, out):
    nc = tc.nc
    with (
        tc.tile_pool(name="consts", bufs=1) as consts,
        tc.tile_pool(name="keep", bufs=1) as keep,
        tc.tile_pool(name="stream", bufs=2) as stream,
        tc.psum_pool(name="psum", bufs=1) as psum,
        tc.manual_schedule(),
    ):
        x_codes = keep.tile([P, PASSES, D], U32, align_bytes=64)
        x_scales = keep.tile([P, PASSES, D], U8, align_bytes=64)
        dp_codes = keep.tile([P, PASSES, H * DH], U32, align_bytes=64)
        dp_scales = keep.tile([P, PASSES, H * DH], U8, align_bytes=64)

        tiles = {}
        pairs = [(HEADS * s + h, s, h, slice(DH * h, DH * h + DH)) for h in range(HEADS) for s in range(SLOTS)]

        def dp_cols(k):
            return slice(CHUNK * (k // PASSES), CHUNK * (k // PASSES) + CHUNK)

        def load_x(c):
            x_rows = stream.tile([P, SLOTS, D], BF16)
            for p0, parts, b, n0, n1 in token_rows(c):
                nc.sync.dma_start(
                    out=x_rows[p0 : p0 + parts], in_=x[b, n0:n1, :].rearrange("(p s) d -> p s d", s=SLOTS)
                )
            tiles["x_rows", c] = x_rows

        def regroup_x(i, copy):
            n_cols = slice(N_TILE * (i % N_TILES), N_TILE * (i % N_TILES) + N_TILE)
            x_grouped = stream.tile([P, N_TILE * SLOTS], BF16, align_bytes=64, bufs=3)
            copy(
                out=x_grouped[:].rearrange("p (c i s) -> p c s i", i=2 * RUN, s=SLOTS),
                in_=tiles["x_rows", i // N_TILES][:, :, n_cols].rearrange("p s (c i) -> p c s i", i=2 * RUN),
            )
            tiles["x_grouped", i] = x_grouped

        def regroup_x_scalar(i):
            regroup_x(i, nc.scalar.copy)

        def quantise_x(i):
            n_cols = slice(N_TILE * (i % N_TILES), N_TILE * (i % N_TILES) + N_TILE)
            nc.vector.quantize_mx(
                out=x_codes[:, i // N_TILES, n_cols].bitcast(E4M3X4),
                scales=x_scales[:, i // N_TILES, n_cols],
                in_=tiles["x_grouped", i][:],
            )

        def load_p(k):
            p = stream.tile([P, SLOTS, CHUNK], F32, bufs=8)
            for p0, parts, b, n0, n1 in token_rows(k % PASSES):
                nc.sync.dma_start(
                    out=p[p0 : p0 + parts], in_=p_x[b, n0:n1, dp_cols(k)].rearrange("(p s) k -> p s k", s=SLOTS)
                )
            tiles["p", k] = p

        def load_g(k):
            h0 = HEADS * (k // PASSES)
            g = stream.tile([P, HEADS, SLOTS, R], BF16, bufs=3)
            for p0, parts, b, n0, n1 in token_rows(k % PASSES):
                nc.sync.dma_start(
                    out=g[p0 : p0 + parts],
                    in_=grad_out[b, h0 : h0 + HEADS, n0:n1, :].rearrange("h (p s) k -> p h s k", s=SLOTS),
                )
            tiles["g", k] = g

        def sum_squares(k):
            norm2 = stream.tile([P, GROUPS], F32, bufs=3)
            squares = stream.tile([P, SLOTS, CHUNK], BF16)
            for i, s, h, cols in pairs:
                nc.scalar.activation(
                    out=squares[:, s, cols], in_=tiles["p", k][:, s, cols], func=ACT.Square, accum_out=norm2[:, i : i + 1]
                )
            tiles["norm2", k] = norm2

        def clamp_norm(k):
            minus_inv = stream.tile([P, GROUPS], F32, bufs=6)
            nc.vector.tensor_scalar(
                out=minus_inv[:], in0=tiles["norm2", k][:], scalar1=EPS * EPS, scalar2=-1.0, op0=ALU.max, op1=ALU.mult
            )
            tiles["minus_inv", k] = minus_inv

        def invert_norm(k):
            nc.vector.reciprocal(out=tiles["minus_inv", k][:], in_=tiles["minus_inv", k][:])

        def root(k):
            rho = stream.tile([P, GROUPS], F32)
            nc.scalar.activation(out=rho[:], in_=tiles["minus_inv", k][:], func=ACT.Sqrt, scale=-1.0)
            tiles["rho", k] = rho

        def fold_gain(u):
            r, kind = u // KINDS, u % KINDS
            folded = stream.tile([P, HEADS, SLOTS * P], F32)
            for h in range(HEADS):
                gain_h = gain_t[:, HEADS * r + h : HEADS * r + h + 1]
                if u == 0:
                    nc.vector.tensor_scalar(
                        out=folded[:, h, :], in0=table_t[:, kind, :], scalar1=gain_h, scalar2=None, op0=ALU.mult
                    )
                else:
                    nc.scalar.activation(out=folded[:, h, :], in_=table_t[:, kind, :], func=ACT.Copy, scale=gain_h)
            tiles["folded", u] = folded

        def lay_table(u):
            for h in range(HEADS):
                tab = psum.tile([P, SLOTS * R], F32, name="tab_%d" % h)
                for s in range(SLOTS):
                    nc.tensor.transpose(
                        out=tab[:, R * s : R * s + R], in_=tiles["folded", u][:, h, P * s : P * s + P], identity=ident[:]
                    )
                tiles["tab", u, h] = tab

        def turn(k):
            u = KINDS * (k // PASSES) + (1 if k % PASSES == B else 0)
            turned = stream.tile([P, SLOTS, HEADS, R], F32)
            for i, s, h, cols in pairs:
                nc.vector.scalar_tensor_tensor(
                    out=turned[:, s, h, :],
                    in0=tiles["g", k][:, h, s, :],
                    scalar=tiles["rho", k][:, i : i + 1],
                    in1=tiles["tab", u, h][:, R * s : R * s + R],
                    op0=ALU.mult,
                    op1=ALU.mult,
                )
            tiles["turned", k] = turned

        def add_halves(k):
            dv = stream.tile([P, SLOTS, CHUNK], F32, bufs=4)
            turned = tiles["turned", k]
            nc.vector.tensor_tensor(
                out=dv[:].rearrange("p s (h j) -> p s h j", h=HEADS),
                in0=turned[:, :, :, 0:DH],
                in1=turned[:, :, :, DH:R],
                op=ALU.add,
            )
            tiles["dv", k] = dv

        def times_p(k):
            prod = stream.tile([P, SLOTS, CHUNK], F32)
            engine = nc.vector if k == CHUNKS - 1 else nc.gpsimd
            if k in TURNED_SUMS:
                engine.tensor_tensor(
                    out=prod[:].rearrange("p s c -> p (s c)").rearrange("p (b g a) -> p g b a", b=DH // SUB, a=SUB),
                    in0=tiles["p", k][:].rearrange("p s (h b a) -> p (s h) b a", h=HEADS, a=SUB),
                    in1=tiles["dv", k][:].rearrange("p s (h b a) -> p (s h) b a", h=HEADS, a=SUB),
                    op=ALU.mult,
                )
            else:
                engine.tensor_tensor(out=prod[:], in0=tiles["p", k][:], in1=tiles["dv", k][:], op=ALU.mult)
            tiles["prod", k] = prod

        def tensor_sums(k):
            sums = sums_bank[:, k % 4, :]
            stretches = tiles["prod", k][:].rearrange("p s (h a b) -> p (s h) a b", a=DH // SUB, b=SUB)
            for a0 in range(DH // SUB):
                nc.tensor.matmul(
                    out=sums.rearrange("p (g b) -> p g b", b=SUB),
                    lhsT=ident[:],
                    rhs=stretches[:, :, a0, :],
                    start=(a0 == 0),
                    stop=(a0 == DH // SUB - 1),
                )
            tiles["sums", k] = sums

        def scale_sums(k):
            whole = stream.tile([P, GROUPS], F32, bufs=3)
            nc.vector.tensor_reduce(
                out=whole[:], in_=tiles["sums", k].rearrange("p (g b) -> p g b", b=SUB), axis=mybir.AxisListType.X, op=ALU.add
            )
            tiles["whole", k] = whole

        def finish_sums(k):
            back = stream.tile([P, GROUPS], F32, name="back", bufs=3)
            nc.vector.tensor_tensor(out=back[:], in0=tiles["whole", k][:], in1=tiles["minus_inv", k][:], op=ALU.mult)
            tiles["back", k] = back

        def turned_sums(k):
            sums_t = sums_bank[:, k % 4, :]
            flat = tiles["prod", k][:].rearrange("p s c -> p (s c)")
            for b0 in range(DH // SUB):
                nc.tensor.matmul(
                    out=sums_t,
                    lhsT=flat[:, P * b0 : P * b0 + P],
                    rhs=ident[:],
                    is_transpose=True,
                    start=(b0 == 0),
                    stop=(b0 == DH // SUB - 1),
                )

        def copy_sums(k):
            sums_sb = stream.tile([P, P], F32)
            nc.scalar.copy(out=sums_sb[:], in_=sums_bank[:, k % 4, :])
            tiles["sums_sb", k] = sums_sb

        def select_sums(k):
            nc.tensor.matmul(out=sums_bank[:, k % 4, 0:GROUPS], lhsT=tiles["sums_sb", k][:], rhs=sel[:], start=True, stop=True)

        def finish_turned(k):
            back = stream.tile([P, GROUPS], F32, name="back", bufs=3)
            nc.vector.tensor_tensor(
                out=back[:], in0=tiles["minus_inv", k][:], in1=sums_bank[:, k % 4, 0:GROUPS], op=ALU.mult
            )
            tiles["back", k] = back

        def project(k):
            along = stream.tile([P, SLOTS, CHUNK], F32)
            for i, s, h, cols in pairs:
                nc.scalar.activation(
                    out=along[:, s, cols], in_=tiles["p", k][:, s, cols], func=ACT.Copy, scale=tiles["back", k][:, i : i + 1]
                )
            tiles["along", k] = along

        def round_dp(k):
            dp = stream.tile([P, CHUNK * SLOTS], BF16, align_bytes=64)
            nc.vector.tensor_tensor(
                out=dp[:].rearrange("p (c i s) -> p c s i", i=2 * RUN, s=SLOTS),
                in0=tiles["dv", k][:].rearrange("p s (c i) -> p c s i", i=2 * RUN),
                in1=tiles["along", k][:].rearrange("p s (c i) -> p c s i", i=2 * RUN),
                op=ALU.add,
            )
            tiles["dp", k] = dp

        def quantise_dp(k):
            nc.vector.quantize_mx(
                out=dp_codes[:, k % PASSES, dp_cols(k)].bitcast(E5M2X4),
                scales=dp_scales[:, k % PASSES, dp_cols(k)],
                in_=tiles["dp", k][:],
            )

        def mx_pass(q, c, bank):
            if c == 0:
                tiles["sum", q] = psum.tile([P, N_TILE], F32, name=bank)
            row0 = P * (q // N_TILES)
            n_cols = slice(N_TILE * (q % N_TILES), N_TILE * (q % N_TILES) + N_TILE)
            nc.tensor.matmul_mx(
                out=tiles["sum", q][:],
                lhsT=dp_codes[:, c, row0 : row0 + P].bitcast(E5M2X4),
                lhsT_scale=dp_scales[:, c, row0 : row0 + P],
                rhs=x_codes[:, c, n_cols].bitcast(E4M3X4),
                rhs_scale=x_scales[:, c, n_cols],
                start=(c == 0),
                stop=(c == PASSES - 1),
            )

        def store_group(q, copy):
            row0 = P * (q // N_TILES)
            n_cols = slice(N_TILE * (q % N_TILES), N_TILE * (q % N_TILES) + N_TILE)
            result = stream.tile([P, N_TILE], F32, bufs=4)
            copy(out=result[:], in_=tiles["sum", q][:])
            nc.sync.dma_start(out=out[row0 : row0 + P, n_cols], in_=result[:])

        per_round = M_TILES * N_TILES
        free_banks = ["acc_0", "acc_1", "acc_2"]
        open_groups = []
        waiting = list(range(per_round * ROUNDS))
        full = []

        def pass_step(q, c):
            return max(PASSES * (q // per_round) + c + 4, 2 * c)

        def empty_banks():
            for q, bank in full:
                store_group(q, nc.scalar.copy)
                free_banks.append(bank)
            full.clear()

        def multiply(last_step):
            while free_banks and waiting:
                open_groups.append([waiting.pop(0), free_banks.pop(0), 0])
            for group in list(open_groups):
                while group[2] < PASSES and pass_step(group[0], group[2]) <= last_step:
                    mx_pass(group[0], group[2], group[1])
                    group[2] += 1
                if group[2] == PASSES:
                    full.append([group[0], group[1]])
                    open_groups.remove(group)

        def when_live(stage, k, count):
            if 0 <= k < count:
                stage(k)

        def step(t):
            when_live(load_p, t + 5, CHUNKS)
            if t % 2 == 0:
                when_live(load_x, t // 2 + 2, PASSES)
            when_live(load_g, t + 2, CHUNKS)

            if t > 0:
                when_live(root, t + 1, CHUNKS)
            empty_banks()
            if t - 2 in TURNED_SUMS:
                select_sums(t - 2)
            if t == CHUNKS:
                free_banks.extend(["tab_%d" % h for h in range(HEADS)])
            multiply(t - 1)

            when_live(sum_squares, t + 3, CHUNKS)
            when_live(regroup_x_scalar, t + 2, PASSES * N_TILES)

            when_live(turn, t, CHUNKS)
            if t - 2 in TURNED_SUMS:
                finish_turned(t - 2)
            else:
                when_live(scale_sums, t - 2, CHUNKS)

            if t % PASSES >= B - 1:
                when_live(lay_table, KINDS * (t // PASSES) + t % PASSES - B + 2, KINDS * ROUNDS)
            if t - 1 in TURNED_SUMS:
                turned_sums(t - 1)
            else:
                when_live(tensor_sums, t - 1, CHUNKS)

            when_live(quantise_dp, t - 4, CHUNKS)
            when_live(clamp_norm, t + 2, CHUNKS)
            when_live(round_dp, t - 3, CHUNKS)
            if t - 2 not in TURNED_SUMS:
                when_live(finish_sums, t - 2, CHUNKS)
            when_live(project, t - 2, CHUNKS)
            when_live(quantise_x, t + 1, PASSES * N_TILES) if t + 1 >= 2 else None
            if B - 2 <= t % PASSES < B:
                when_live(fold_gain, KINDS * (t // PASSES) + t % PASSES - B + 3, KINDS * ROUNDS)
            if t - 1 in TURNED_SUMS:
                copy_sums(t - 1)
            when_live(add_halves, t, CHUNKS)
            when_live(times_p, t, CHUNKS)
            when_live(invert_norm, t + 2, CHUNKS)

            if t >= CHUNKS:
                multiply(t)

        sums_bank = psum.tile([P, 4, GROUPS * SUB], F32)
        warm = consts.tile([P, 2], F32)
        nc.vector.memset(warm[:, 0:1], 0.0)
        nc.scalar.activation(out=warm[:, 1:2], in_=warm[:, 0:1], func=ACT.Sin)
        gain_rows = consts.tile([P, R], BF16)
        nc.vector.memset(gain_rows[:], 0.0)
        for half in range(2):
            nc.sync.dma_start(
                out=gain_rows[0:H, DH * half : DH * half + DH], in_=qx_scale.rearrange("h o j -> h (o j)")
            )
        load_p(0)
        load_x(0)
        load_g(0)
        load_p(1)
        load_x(1)
        load_p(2)
        load_g(1)
        load_p(3)
        load_p(4)
        kinds = KINDS * SLOTS
        pos_int = consts.tile([P, KINDS, SLOTS], I32)
        nc.gpsimd.iota(pos_int[:, 0, :], pattern=[[1, SLOTS]], base=0, channel_multiplier=SLOTS)
        ident = consts.tile([P, P], F32)
        masks.make_identity(nc, ident[:])
        nc.vector.tensor_single_scalar(
            out=pos_int[:, 1, :], in_=pos_int[:, 0, :], scalar=SLOTS * REST_P - 1, op=ALU.bitwise_and
        )
        pos = consts.tile([P, KINDS, SLOTS], F32)
        nc.vector.tensor_copy(out=pos[:, 0, :], in_=pos_int[:, 0, :])
        nc.vector.tensor_scalar(
            out=pos[:, 1, :], in0=pos_int[:, 1, :], scalar1=float(MAIN_N), scalar2=None, op0=ALU.add
        )
        theta = consts.tile([P, kinds, DH], F32)
        for j in range(DH):
            if j % 2 == 0:
                nc.vector.tensor_scalar(
                    out=theta[:, :, j],
                    in0=pos[:].rearrange("p k s -> p (k s)"),
                    scalar1=1.0 / (BASE ** (2 * j / R)),
                    scalar2=None,
                    op0=ALU.mult,
                )
            else:
                nc.scalar.activation(
                    out=theta[:, :, j],
                    in_=pos[:].rearrange("p k s -> p (k s)"),
                    func=ACT.Copy,
                    scale=1.0 / (BASE ** (2 * j / R)),
                )
        sum_squares(0)
        turns = consts.tile([P, kinds, DH], F32)
        nc.vector.tensor_scalar(
            out=turns[:], in0=theta[:], scalar1=1.0 / (2.0 * math.pi), scalar2=ROUND_MAGIC, op0=ALU.mult, op1=ALU.add
        )
        gain_f32 = consts.tile([P, R], F32)
        nc.vector.tensor_copy(out=gain_f32[:], in_=gain_rows[:])
        nc.vector.tensor_scalar(out=turns[:], in0=turns[:], scalar1=ROUND_MAGIC, scalar2=None, op0=ALU.subtract)
        rem = consts.tile([P, kinds, DH], F32)
        nc.vector.scalar_tensor_tensor(
            out=rem[:], in0=turns[:], scalar=-TWO_PI_HI, in1=theta[:], op0=ALU.mult, op1=ALU.add
        )
        nc.vector.scalar_tensor_tensor(
            out=rem[:], in0=turns[:], scalar=-TWO_PI_LO, in1=rem[:], op0=ALU.mult, op1=ALU.add
        )
        nc.vector.tensor_scalar(out=rem[:], in0=rem[:], scalar1=-PI_INSIDE, scalar2=PI_INSIDE, op0=ALU.max, op1=ALU.min)
        clamp_norm(0)
        quarter = turns
        nc.vector.scalar_tensor_tensor(out=quarter[:], in0=rem[:], scalar=-1.0, in1=rem[:], op0=ALU.mult, op1=ALU.max)
        invert_norm(0)
        nc.vector.tensor_scalar(
            out=quarter[:], in0=quarter[:], scalar1=-1.0, scalar2=math.pi / 2.0, op0=ALU.mult, op1=ALU.add
        )
        cos_sin = consts.tile([P, kinds, R], F32)
        for kind in range(KINDS):
            of_kind = slice(SLOTS * kind, SLOTS * kind + SLOTS)
            nc.scalar.activation(out=cos_sin[:, of_kind, DH:R], in_=rem[:, of_kind, :], func=ACT.Sin)
            nc.scalar.activation(out=cos_sin[:, of_kind, 0:DH], in_=quarter[:, of_kind, :], func=ACT.Sin)
        root(0)

        table_t = consts.tile([P, KINDS, SLOTS * P], F32)
        gain_t = consts.tile([P, H], F32)
        turned_gain = psum.tile([P, P], F32, name="tab_2")
        nc.tensor.transpose(out=turned_gain[:], in_=gain_f32[:], identity=ident[:])
        nc.scalar.copy(out=gain_t[:], in_=turned_gain[:, 0:H])
        for kind in range(KINDS):
            turned_table = psum.tile([P, SLOTS * P], F32, name="tab_%d" % kind)
            for s in range(SLOTS):
                nc.tensor.transpose(
                    out=turned_table[:, P * s : P * s + P], in_=cos_sin[:, SLOTS * kind + s, :], identity=ident[:]
                )
            nc.scalar.copy(out=table_t[:, kind, :], in_=turned_table[:])
            if kind == 0:
                sum_squares(1)
        sum_squares(2)
        regroup_x(0, nc.vector.tensor_copy)
        regroup_x(1, nc.vector.tensor_copy)
        fold_gain(0)
        lay_table(0)
        quantise_x(0)
        clamp_norm(1)
        quantise_x(1)
        invert_norm(1)
        root(1)
        sel = consts.tile([P, GROUPS], F32)
        nc.vector.tensor_reduce(
            out=sel[:], in_=ident[:].rearrange("p (g b) -> p g b", b=SUB), axis=mybir.AxisListType.X, op=ALU.add
        )
        for t in range(0, CHUNKS + 4):
            step(t)
        for q, bank in full:
            store_group(q, nc.scalar.copy if q % 2 == 0 else nc.vector.tensor_copy)
